import numpy as np
import ml_dtypes


def mxq(x, axis, fmt="e4m3"):
    dtype, down = {"e4m3": (ml_dtypes.float8_e4m3fn, 7), "e5m2": (ml_dtypes.float8_e5m2, 14)}[fmt]
    v = np.moveaxis(np.asarray(x, np.float32).astype(ml_dtypes.bfloat16).astype(np.float64), axis, -1)
    blocks = v.reshape(v.shape[:-1] + (-1, 32))
    amax = np.abs(blocks).max(-1, keepdims=True)
    byte = np.maximum(np.where(amax > 0, np.frexp(amax)[1] - 1 + 127, 0) - down, 1)
    scale = np.exp2(byte - 127.0)
    codes = (blocks / scale).astype(np.float32).astype(dtype).astype(np.float64)
    return np.moveaxis((codes * scale).reshape(v.shape), -1, axis)


WIDE = False


def mx_kscale(k):
    if not WIDE:
        return np.ones(k)
    levels = np.array([10, -10, 5, -5, 0])
    if k % 512:
        return np.exp2(np.random.permutation(np.resize(levels, k // 32))).repeat(32)
    a = np.empty((k // 512, 16))
    for p in range(k // 512):
        a[p, :8] = np.random.permutation(np.resize(levels, 8))
        for g in range(8):
            far = levels[np.abs(levels - a[p, g]) >= 10]
            a[p, g + 8] = far[np.random.randint(len(far))]
    return np.exp2(a.ravel()).repeat(32)


BF16 = ml_dtypes.bfloat16


def bf(x):
    return np.asarray(x, np.float32).astype(BF16)


def f64(x):
    return np.asarray(x).astype(np.float64)


B, C, CK, CV, CO, H, W, P1, P2, P3, P4 = 2, 1024, 1024, 128, 1024, 48, 48, 1, 3, 6, 8
PSP_SIZES = (P1, P2, P3, P4)
EPS = 1e-5
N = H * W


def bnrelu(x, gamma, beta, mean, var):
    inv = 1.0 / np.sqrt(var + EPS)
    return np.maximum((x - mean[None, :, None]) * (inv * gamma)[None, :, None] + beta[None, :, None], 0.0)


def psp(x):
    b, c = x.shape[:2]
    outs = []
    for s in PSP_SIZES:
        outs.append(x.reshape(b, c, s, H // s, s, W // s).mean(axis=(3, 5)).reshape(b, c, s * s))
    return np.concatenate(outs, axis=-1)


def setup_inputs():
    s = mx_kscale(C)
    fine = np.random.standard_normal((B, C, H, W))
    coarse = np.random.standard_normal((B, C, P4, P4))
    coarse = np.repeat(np.repeat(coarse, H // P4, axis=2), W // P4, axis=3)
    return {"feats": bf((fine + coarse) * np.sqrt(0.5) * s[None, :, None, None]),
            "Wk": bf(np.random.standard_normal((CK, C)) * 1.5 / np.sqrt(C) / s[None, :]),
            "bk": bf(np.random.standard_normal(CK) * 0.2),
            "gk": bf(1.0 + 0.1 * np.random.standard_normal(CK)),
            "betak": bf(np.random.standard_normal(CK) * 0.2),
            "mk": bf(np.random.standard_normal(CK) * 0.2),
            "vk": bf(np.random.uniform(0.5, 1.5, CK)),
            "Wv": bf(np.random.standard_normal((CV, C)) / np.sqrt(C) / s[None, :]),
            "bv": bf(np.random.standard_normal(CV) * 0.2)}


def reference(feats, Wk, bk, gk, betak, mk, vk, Wv, bv):
    xq = mxq(f64(feats).reshape(B, C, N), 1, "e4m3")
    pre = (mxq(f64(Wk), 1, "e4m3") @ xq) + f64(bk)[None, :, None]
    kf = bnrelu(pre, f64(gk), f64(betak), f64(mk), f64(vk)).reshape(B, CK, H, W)
    keyp = psp(kf)
    val = ((mxq(f64(Wv), 1, "e4m3") @ xq) + f64(bv)[None, :, None]).reshape(B, CV, H, W)
    value = psp(val).transpose(0, 2, 1)
    return kf, keyp, value

@@ -1,0 +1,317 @@
+from contextlib import ExitStack
+
+import concourse.mybir as mybir
+from concourse.masks import make_identity
+
+F32 = mybir.dt.float32
+BF16 = mybir.dt.bfloat16
+U32 = mybir.dt.uint32
+U8 = mybir.dt.uint8
+FP8X4 = mybir.dt.float8_e4m3fn_x4
+ACT = mybir.ActivationFunctionType
+ADD = mybir.AluOpType.add
+AXIS = mybir.AxisListType
+
+P = 128
+PACK = 4
+PASSES = 2
+IMAGES = 2
+SIDE = 48
+HALF_ROWS = 24
+HALF = HALF_ROWS * SIDE
+HALVES = 2 * IMAGES
+KEY_TILES = 8
+VALUE_TILE = 8
+TILES = KEY_TILES + 1
+BANK = 512
+QUANT_MAX = 4096
+BLOCKS = 3
+BLOCK = HALF // BLOCKS
+TOKENS = 110
+AT3, AT6, AT8 = 1, 10, 46
+EPS = 1e-5
+
+FLOPS = 2 * IMAGES * SIDE * SIDE * 1024 * (1024 + 128)
+
+
+def tile_apnb_pa_t_kernel(
+    tc, feats, Wk, bk, gk, betak, mk, vk, Wv, bv, out_0, out_1, out_2
+):
+    nc = tc.nc
+
+    x_view = feats.rearrange("b (g q u e) h w -> b q g u e (h w)", g=PASSES, u=2, e=2)
+    kf_view = out_0.rearrange("b (p m) h w -> b p m (h w)", m=KEY_TILES)
+    keyp_view = out_1.rearrange("b (p m) t -> b p (m t)", m=KEY_TILES)
+
+    with ExitStack() as ctx:
+        consts = ctx.enter_context(tc.tile_pool(name="consts", bufs=1))
+        xraw_pool = ctx.enter_context(tc.tile_pool(name="xraw", bufs=3))
+        grouped_pool = ctx.enter_context(tc.tile_pool(name="grouped", bufs=3))
+        xq_pool = ctx.enter_context(tc.tile_pool(name="xq", bufs=2))
+        wstage = ctx.enter_context(tc.tile_pool(name="wstage", bufs=2))
+        kf_pool = ctx.enter_context(tc.tile_pool(name="kf", bufs=3))
+        pool_tmp = ctx.enter_context(tc.tile_pool(name="pool_tmp", bufs=2))
+        sums_pool = ctx.enter_context(tc.tile_pool(name="sums", bufs=2))
+        psum = ctx.enter_context(tc.psum_pool(name="psum", bufs=7))
+
+        ident = consts.tile([P, P], F32)
+        make_identity(nc, ident[:])
+
+        prm = consts.tile([P, 6, 16], BF16)
+        with nc.allow_non_contiguous_dma(reason="8 channels (16 bytes) to a partition"):
+            for slot, vec in enumerate((bk, gk, betak, mk, vk)):
+                nc.scalar.dma_start(
+                    out=prm[:, slot, 0:KEY_TILES],
+                    in_=vec.rearrange("(p m) -> p m", m=KEY_TILES),
+                )
+            nc.scalar.dma_start(out=prm[:, 5, 0:1], in_=bv.rearrange("(p o) -> p o", o=1))
+
+        xraw = {}
+
+        def load_x(half, piece, start=0, width=HALF):
+            if half not in xraw:
+                xraw[half] = xraw_pool.tile([P, PASSES, PACK, HALF], BF16, name="xraw")
+            g, u = divmod(piece, 2)
+            first = (half % 2) * HALF
+            nc.sync.dma_start(
+                out=xraw[half][:, g, 2 * u : 2 * u + 2, start : start + width],
+                in_=x_view[half // 2, :, g, u, :, first + start : first + start + width],
+            )
+
+        wv_raw = consts.tile([P, 1024], BF16)
+        for g in range(PASSES):
+            for block in range(BLOCKS):
+                for u in range(2):
+                    load_x(0, 2 * g + u, block * BLOCK, BLOCK)
+            if g == 0:
+                nc.sync.dma_start(out=wv_raw[:], in_=Wv)
+        wk_raw = consts.tile([P, KEY_TILES, 1024], BF16)
+        wk_view = Wk.rearrange("(p m) k -> p m k", m=KEY_TILES)
+        for m in range(0, KEY_TILES, 2):
+            nc.sync.dma_start(out=wk_raw[:, m : m + 2, :], in_=wk_view[:, m : m + 2, :])
+        for piece in range(4):
+            load_x(1, piece)
+
+        scale_t = consts.tile([P, TILES], F32)
+        bias_t = consts.tile([P, TILES], F32)
+        std = consts.tile([P, KEY_TILES], F32)
+        keys = slice(0, KEY_TILES)
+        nc.vector.tensor_scalar_add(out=std[:], in0=prm[:, 4, keys], scalar1=EPS)
+        nc.scalar.sqrt(out=std[:], in_=std[:])
+        nc.vector.reciprocal(out=std[:], in_=std[:])
+        nc.vector.tensor_mul(out=scale_t[:, keys], in0=std[:], in1=prm[:, 1, keys])
+        nc.vector.tensor_sub(out=bias_t[:, keys], in0=prm[:, 0, keys], in1=prm[:, 3, keys])
+        nc.vector.tensor_mul(out=bias_t[:, keys], in0=bias_t[:, keys], in1=scale_t[:, keys])
+        nc.vector.tensor_add(out=bias_t[:, keys], in0=bias_t[:, keys], in1=prm[:, 2, keys])
+        nc.vector.memset(scale_t[:, VALUE_TILE : VALUE_TILE + 1], 1.0)
+        nc.vector.tensor_copy(out=bias_t[:, VALUE_TILE : VALUE_TILE + 1], in_=prm[:, 5, 0:1])
+
+        grouped = {}
+        x_codes = {}
+        x_scales = {}
+
+        def regroup_x(half, g, block, copy):
+            if block == 0:
+                grouped[half, g] = grouped_pool.tile(
+                    [P, HALF, PACK], BF16, name="grouped", align_bytes=64
+                )
+            cols = slice(block * BLOCK, (block + 1) * BLOCK)
+            copy(
+                out=grouped[half, g][:, cols, :].rearrange("p (c i) t -> p c t i", i=4),
+                in_=xraw[half][:, g, :, cols].rearrange("p t (c i) -> p c t i", i=4),
+            )
+
+        def quantise_x(half, g):
+            if g == 0:
+                x_codes[half] = xq_pool.tile([P, PASSES, HALF], U32, name="x_codes", align_bytes=64)
+                x_scales[half] = xq_pool.tile([P, PASSES, HALF], U8, name="x_scales", align_bytes=64)
+            flat = grouped[half, g][:].rearrange("p n t -> p (n t)")
+            for first in range(0, HALF * PACK, QUANT_MAX):
+                width = min(QUANT_MAX, HALF * PACK - first)
+                words = slice(first // PACK, (first + width) // PACK)
+                nc.vector.quantize_mx(
+                    out=x_codes[half][:, g, words].bitcast(FP8X4),
+                    scales=x_scales[half][:, g, words],
+                    in_=flat[:, first : first + width],
+                )
+
+        w_codes = consts.tile([P, TILES, PASSES * P], U32, align_bytes=64)
+        w_scales = consts.tile([P, TILES, PASSES * P], U8, align_bytes=64)
+
+        def prepare_weights(m):
+            rows = wv_raw[:] if m == VALUE_TILE else wk_raw[:, m, :]
+            words = rows.bitcast(F32)
+            turned = psum.tile([P, BANK], F32, tag="acc")
+            for gu in range(PASSES * 2):
+                g, u = divmod(gu, 2)
+                nc.tensor.transpose(
+                    turned[:, gu * P : (gu + 1) * P],
+                    words[:, g * 2 * P + u : (g + 1) * 2 * P : 2],
+                    ident[:],
+                )
+            w_grouped = wstage.tile([P, PASSES, P, PACK], BF16, align_bytes=64)
+            nc.scalar.copy(
+                out=w_grouped[:].bitcast(F32),
+                in_=turned[:].rearrange("q (g u c) -> q g c u", g=PASSES, u=2),
+            )
+            nc.vector.quantize_mx(
+                out=w_codes[:, m, :].bitcast(FP8X4),
+                scales=w_scales[:, m, :],
+                in_=w_grouped[:].rearrange("q g c t -> q (g c t)"),
+            )
+
+        def project(half, tiles):
+            kf = kf_pool.tile([P, len(tiles), HALF], F32, name="kf")
+            for j, m in enumerate(tiles):
+                for first in range(0, HALF, BANK):
+                    width = min(BANK, HALF - first)
+                    acc = psum.tile([P, BANK], F32, tag="acc")
+                    for g in range(PASSES):
+                        nc.tensor.matmul_mx(
+                            out=acc[:, 0:width],
+                            lhsT=w_codes[:, m, g * P : (g + 1) * P].bitcast(FP8X4),
+                            lhsT_scale=w_scales[:, m, g * P : (g + 1) * P],
+                            rhs=x_codes[half][:, g, first : first + width].bitcast(FP8X4),
+                            rhs_scale=x_scales[half][:, g, first : first + width],
+                            start=(g == 0),
+                            stop=(g == PASSES - 1),
+                        )
+                    nc.scalar.activation(
+                        out=kf[:, j, first : first + width],
+                        in_=acc[:, 0:width],
+                        func=ACT.Identity if m == VALUE_TILE else ACT.Relu,
+                        bias=bias_t[:, m : m + 1],
+                        scale=scale_t[:, m : m + 1],
+                    )
+            if tiles[0] != VALUE_TILE:
+                first = (half % 2) * HALF
+                nc.sync.dma_start(
+                    out=kf_view[half // 2, :, tiles[0] : tiles[0] + len(tiles), first : first + HALF],
+                    in_=kf[:],
+                )
+            return kf
+
+        sums8 = {}
+        sums6 = {}
+
+        def add_row_pairs(work):
+            kf = work["kf"]
+            pairs = pool_tmp.tile([P, len(work["tiles"]) * HALF_ROWS // 2, SIDE], F32, name="row_pairs")
+            rows = kf[:].rearrange("p n (a two w) -> p (n a) two w", two=2, w=SIDE)
+            nc.vector.tensor_tensor(out=pairs[:], in0=rows[:, :, 0, :], in1=rows[:, :, 1, :], op=ADD)
+            work["row_pairs"] = pairs
+
+        def add_column_pairs(work):
+            pairs = work["row_pairs"]
+            quads = pool_tmp.tile([P, len(work["tiles"]) * HALF // 4], F32, name="quads")
+            cols = pairs[:].rearrange("p a (c two) -> p (a c) two", two=2)
+            nc.vector.tensor_tensor(out=quads[:], in0=cols[:, :, 0], in1=cols[:, :, 1], op=ADD)
+            work["quads"] = quads
+
+        def sum_cells(work):
+            half, tiles, quads = work["half"], work["tiles"], work["quads"]
+            b, part = divmod(half, 2)
+            if part == 0 and tiles[0] == VALUE_TILE:
+                sums8[b] = sums_pool.tile([P, 2, TILES, 32], F32, name="sums8")
+                sums6[b] = sums_pool.tile([P, 2, TILES, 18], F32, name="sums6")
+            span = slice(tiles[0], tiles[0] + len(tiles))
+            nc.vector.tensor_reduce(
+                out=sums8[b][:, part, span, :].rearrange("p n (r c) -> p (n r) c", c=8),
+                in_=quads[:].rearrange("p (r hi c wi) -> p r c hi wi", hi=3, c=8, wi=3),
+                axis=AXIS.XY,
+                op=ADD,
+            )
+            nc.vector.tensor_reduce(
+                out=sums6[b][:, part, span, :].rearrange("p n (r c) -> p (n r) c", c=6),
+                in_=quads[:].rearrange("p (r hi c wi) -> p r c hi wi", hi=4, c=6, wi=4),
+                axis=AXIS.XY,
+                op=ADD,
+            )
+
+        def finish_image(b):
+            tok = sums_pool.tile([P, KEY_TILES * TOKENS + P], F32, name="tok")
+            nc.vector.memset(tok[:, KEY_TILES * TOKENS :], 0.0)
+            by_tile = tok[:, 0 : TILES * TOKENS].rearrange("p (m t) -> p m t", t=TOKENS)
+            level8 = by_tile[:, :, AT8:TOKENS]
+            level6 = by_tile[:, :, AT6:AT8]
+            nc.scalar.mul(
+                out=level6.rearrange("p m (h j) -> p h m j", h=2), in_=sums6[b][:], mul=1.0 / 64.0
+            )
+            nc.scalar.mul(
+                out=level8.rearrange("p m (h j) -> p h m j", h=2), in_=sums8[b][:], mul=1.0 / 36.0
+            )
+            wide = sums_pool.tile([P, TILES, 18], F32, name="wide")
+            nc.vector.tensor_reduce(
+                out=wide[:], in_=level6.rearrange("p m (a wi) -> p m a wi", wi=2), axis=AXIS.X, op=ADD
+            )
+            cells3 = sums_pool.tile([P, TILES * 3, 3], F32, name="cells3")
+            nc.vector.tensor_reduce(
+                out=cells3[:],
+                in_=wide[:].rearrange("p m (r hi c) -> p (m r) c hi", hi=2, c=3),
+                axis=AXIS.X,
+                op=ADD,
+            )
+            nine = cells3[:].rearrange("p (m r) c -> p m (r c)", m=TILES)
+            nc.scalar.mul(out=by_tile[:, :, AT3:AT6], in_=nine, mul=0.25)
+            whole = sums_pool.tile([P, TILES], F32, name="whole")
+            nc.vector.tensor_reduce(out=whole[:], in_=nine, axis=AXIS.X, op=ADD)
+            nc.scalar.mul(out=by_tile[:, :, 0:AT3], in_=whole[:].unsqueeze(2), mul=1.0 / 36.0)
+            nc.sync.dma_start(out=keyp_view[b], in_=tok[:, 0 : KEY_TILES * TOKENS])
+            return tok
+
+        def store_value(b, tok):
+            turned = psum.tile([P, P], F32, tag="value", bufs=1)
+            nc.tensor.transpose(turned[:], tok[:, KEY_TILES * TOKENS :], ident[:])
+            value = sums_pool.tile([P, P], F32, name="value")
+            nc.scalar.copy(out=value[:], in_=turned[:])
+            nc.sync.dma_start(out=out_2[b], in_=value[0:TOKENS, :])
+
+        groups = [[VALUE_TILE]] + [[m, m + 1] for m in range(0, KEY_TILES, 2)]
+        tile_order = [m for tiles in groups for m in tiles]
+
+        for g in range(PASSES):
+            regroup_x(0, g, 0, nc.vector.tensor_copy)
+            regroup_x(0, g, 1, nc.vector.tensor_copy)
+            regroup_x(0, g, 2, nc.scalar.copy)
+            if g > 0:
+                quantise_x(0, g - 1)
+        prepare_weights(tile_order[0])
+        quantise_x(0, PASSES - 1)
+
+        previous = None
+        value_due = None
+        for half in range(HALVES):
+            following = half + 1
+            for step, tiles in enumerate(groups):
+                if half == 0 and step + 1 < len(groups):
+                    for m in groups[step + 1]:
+                        prepare_weights(m)
+                if half + 2 < HALVES and step < 4:
+                    load_x(half + 2, step)
+                if following < HALVES and step >= 2 and step % 2 == 0:
+                    quantise_x(following, step // 2 - 1)
+
+                work = {"half": half, "tiles": tiles, "kf": project(half, tiles)}
+                if value_due is not None:
+                    store_value(value_due[0], value_due[1])
+                    value_due = None
+
+                if previous is not None:
+                    add_column_pairs(previous)
+                add_row_pairs(work)
+                if previous is not None:
+                    sum_cells(previous)
+                    if previous["half"] % 2 == 1 and previous["tiles"] == groups[-1]:
+                        b = previous["half"] // 2
+                        value_due = (b, finish_image(b))
+                previous = work
+
+                if following < HALVES and step < 2 * PASSES:
+                    g = step // 2
+                    regroup_x(following, g, step % 2, nc.scalar.copy)
+                    if step % 2 == 1:
+                        regroup_x(following, g, 2, nc.vector.tensor_copy)
+
+        add_column_pairs(previous)
+        sum_cells(previous)
+        store_value(IMAGES - 1, finish_image(IMAGES - 1))

@@ -10,6 +10,7 @@ U8 = mybir.dt.uint8
 FP8X4 = mybir.dt.float8_e4m3fn_x4
 ACT = mybir.ActivationFunctionType
 ADD = mybir.AluOpType.add
+MULT = mybir.AluOpType.mult
 AXIS = mybir.AxisListType
 
 P = 128
@@ -27,9 +28,11 @@ BANK = 512
 QUANT_MAX = 4096
 BLOCKS = 3
 BLOCK = HALF // BLOCKS
+QUADS = HALF // 4
 TOKENS = 110
 AT3, AT6, AT8 = 1, 10, 46
 EPS = 1e-5
+LAST_PARTS = ((0, 5), (5, 7), (7, 9))
 
 FLOPS = 2 * IMAGES * SIDE * SIDE * 1024 * (1024 + 128)
 
@@ -41,7 +44,7 @@ def tile_apnb_pa_t_kernel(
 
     x_view = feats.rearrange("b (g q u e) h w -> b q g u e (h w)", g=PASSES, u=2, e=2)
     kf_view = out_0.rearrange("b (p m) h w -> b p m (h w)", m=KEY_TILES)
-    keyp_view = out_1.rearrange("b (p m) t -> b p (m t)", m=KEY_TILES)
+    keyp_view = out_1.rearrange("b (p m) t -> b p m t", m=KEY_TILES)
 
     with ExitStack() as ctx:
         consts = ctx.enter_context(tc.tile_pool(name="consts", bufs=1))
@@ -51,6 +54,8 @@ def tile_apnb_pa_t_kernel(
         wstage = ctx.enter_context(tc.tile_pool(name="wstage", bufs=2))
         kf_pool = ctx.enter_context(tc.tile_pool(name="kf", bufs=3))
         pool_tmp = ctx.enter_context(tc.tile_pool(name="pool_tmp", bufs=2))
+        quads_pool = ctx.enter_context(tc.tile_pool(name="quads", bufs=2))
+        band_pool = ctx.enter_context(tc.tile_pool(name="bands", bufs=1))
         sums_pool = ctx.enter_context(tc.tile_pool(name="sums", bufs=2))
         psum = ctx.enter_context(tc.psum_pool(name="psum", bufs=7))
 
@@ -105,6 +110,14 @@ def tile_apnb_pa_t_kernel(
         nc.vector.tensor_add(out=bias_t[:, keys], in0=bias_t[:, keys], in1=prm[:, 2, keys])
         nc.vector.memset(scale_t[:, VALUE_TILE : VALUE_TILE + 1], 1.0)
         nc.vector.tensor_copy(out=bias_t[:, VALUE_TILE : VALUE_TILE + 1], in_=prm[:, 5, 0:1])
+
+        ones = consts.tile([P, TOKENS], F32)
+        nc.gpsimd.memset(ones[:], 1.0)
+        inv_area = consts.tile([P, TOKENS], F32)
+        for first, last, side in ((0, AT3, 48), (AT3, AT6, 16), (AT6, AT8, 8), (AT8, TOKENS, 6)):
+            nc.vector.tensor_scalar_mul(
+                out=inv_area[:, first:last], in0=ones[:, first:last], scalar1=1.0 / (side * side)
+            )
 
         grouped = {}
         x_codes = {}
@@ -191,8 +204,12 @@ def tile_apnb_pa_t_kernel(
                 )
             return kf
 
-        sums8 = {}
-        sums6 = {}
+        def slot_of(m):
+            return 0 if m == VALUE_TILE else m + 1
+
+        quads_of = {}
+        sums_of = {}
+        tokens_of = {}
 
         def add_row_pairs(work):
             kf = work["kf"]
@@ -202,69 +219,131 @@ def tile_apnb_pa_t_kernel(
             work["row_pairs"] = pairs
 
         def add_column_pairs(work):
-            pairs = work["row_pairs"]
-            quads = pool_tmp.tile([P, len(work["tiles"]) * HALF // 4], F32, name="quads")
+            half, tiles, pairs = work["half"], work["tiles"], work["row_pairs"]
+            if half not in quads_of:
+                quads_of[half] = quads_pool.tile([P, TILES, QUADS], F32, name="quads")
             cols = pairs[:].rearrange("p a (c two) -> p (a c) two", two=2)
-            nc.vector.tensor_tensor(out=quads[:], in0=cols[:, :, 0], in1=cols[:, :, 1], op=ADD)
-            work["quads"] = quads
+            slot = slot_of(tiles[0])
+            span = slice(slot, slot + len(tiles))
+            nc.vector.tensor_tensor(
+                out=quads_of[half][:, span, :].rearrange("p n q -> p (n q)"),
+                in0=cols[:, :, 0],
+                in1=cols[:, :, 1],
+                op=ADD,
+            )
 
-        def sum_cells(work):
-            half, tiles, quads = work["half"], work["tiles"], work["quads"]
+        def cell_sums(half, first, last):
+            n = last - first
             b, part = divmod(half, 2)
-            if part == 0 and tiles[0] == VALUE_TILE:
-                sums8[b] = sums_pool.tile([P, 2, TILES, 32], F32, name="sums8")
-                sums6[b] = sums_pool.tile([P, 2, TILES, 18], F32, name="sums6")
-            span = slice(tiles[0], tiles[0] + len(tiles))
-            nc.vector.tensor_reduce(
-                out=sums8[b][:, part, span, :].rearrange("p n (r c) -> p (n r) c", c=8),
-                in_=quads[:].rearrange("p (r hi c wi) -> p r c hi wi", hi=3, c=8, wi=3),
-                axis=AXIS.XY,
-                op=ADD,
-            )
-            nc.vector.tensor_reduce(
-                out=sums6[b][:, part, span, :].rearrange("p n (r c) -> p (n r) c", c=6),
-                in_=quads[:].rearrange("p (r hi c wi) -> p r c hi wi", hi=4, c=6, wi=4),
-                axis=AXIS.XY,
-                op=ADD,
-            )
+            if b not in sums_of:
+                sums_of[b] = sums_pool.tile([P, TILES, TOKENS], F32, name="sums")
+            quads = quads_of[half][:, first:last, :]
+            sixes = quads.rearrange("p n (i s c) -> p (n i) s c", s=6, c=24)
+            rows = quads.rearrange("p n (a c) -> p n a c", c=24)
+            sums = sums_of[b][:, first:last, :]
+            two = band_pool.tile([P, n, 4, 24], F32, name="two")
+            bands8 = band_pool.tile([P, n, 4, 24], F32, name="bands8")
+            bands6 = band_pool.tile([P, n, 3, 24], F32, name="bands6")
+            split = "p n (i j) c -> p (n i) j c"
 
-        def finish_image(b):
-            tok = sums_pool.tile([P, KEY_TILES * TOKENS + P], F32, name="tok")
-            nc.vector.memset(tok[:, KEY_TILES * TOKENS :], 0.0)
-            by_tile = tok[:, 0 : TILES * TOKENS].rearrange("p (m t) -> p m t", t=TOKENS)
-            level8 = by_tile[:, :, AT8:TOKENS]
-            level6 = by_tile[:, :, AT6:AT8]
-            nc.scalar.mul(
-                out=level6.rearrange("p m (h j) -> p h m j", h=2), in_=sums6[b][:], mul=1.0 / 64.0
-            )
-            nc.scalar.mul(
-                out=level8.rearrange("p m (h j) -> p h m j", h=2), in_=sums8[b][:], mul=1.0 / 36.0
-            )
-            wide = sums_pool.tile([P, TILES, 18], F32, name="wide")
-            nc.vector.tensor_reduce(
-                out=wide[:], in_=level6.rearrange("p m (a wi) -> p m a wi", wi=2), axis=AXIS.X, op=ADD
-            )
-            cells3 = sums_pool.tile([P, TILES * 3, 3], F32, name="cells3")
-            nc.vector.tensor_reduce(
-                out=cells3[:],
-                in_=wide[:].rearrange("p m (r hi c) -> p (m r) c hi", hi=2, c=3),
-                axis=AXIS.X,
-                op=ADD,
-            )
-            nine = cells3[:].rearrange("p (m r) c -> p m (r c)", m=TILES)
-            nc.scalar.mul(out=by_tile[:, :, AT3:AT6], in_=nine, mul=0.25)
-            whole = sums_pool.tile([P, TILES], F32, name="whole")
-            nc.vector.tensor_reduce(out=whole[:], in_=nine, axis=AXIS.X, op=ADD)
-            nc.scalar.mul(out=by_tile[:, :, 0:AT3], in_=whole[:].unsqueeze(2), mul=1.0 / 36.0)
-            nc.sync.dma_start(out=keyp_view[b], in_=tok[:, 0 : KEY_TILES * TOKENS])
-            return tok
+            def add_two():
+                nc.vector.tensor_tensor(
+                    out=two[:].rearrange(split, j=2),
+                    in0=sixes[:, :, 0:5:4, :],
+                    in1=sixes[:, :, 1:6:4, :],
+                    op=ADD,
+                )
 
-        def store_value(b, tok):
-            turned = psum.tile([P, P], F32, tag="value", bufs=1)
-            nc.tensor.transpose(turned[:], tok[:, KEY_TILES * TOKENS :], ident[:])
-            value = sums_pool.tile([P, P], F32, name="value")
-            nc.scalar.copy(out=value[:], in_=turned[:])
-            nc.sync.dma_start(out=out_2[b], in_=value[0:TOKENS, :])
+            def add_third():
+                nc.vector.tensor_tensor(
+                    out=bands8[:].rearrange(split, j=2),
+                    in0=two[:].rearrange(split, j=2),
+                    in1=sixes[:, :, 2:4, :],
+                    op=ADD,
+                )
+
+            def middle_band():
+                nc.vector.tensor_tensor(
+                    out=bands6[:, :, 1, :], in0=two[:, :, 1, :], in1=two[:, :, 2, :], op=ADD
+                )
+
+            def outer_bands():
+                nc.vector.tensor_tensor(
+                    out=bands6[:, :, 0:3:2, :],
+                    in0=bands8[:, :, 0:4:3, :],
+                    in1=rows[:, :, 3:9:5, :],
+                    op=ADD,
+                )
+
+            def level8():
+                nc.vector.tensor_reduce(
+                    out=sums[:, :, AT8 + 32 * part : AT8 + 32 * (part + 1)],
+                    in_=bands8[:].rearrange("p n r (c wi) -> p n (r c) wi", wi=3),
+                    axis=AXIS.X,
+                    op=ADD,
+                )
+
+            def level6():
+                nc.vector.tensor_reduce(
+                    out=sums[:, :, AT6 + 18 * part : AT6 + 18 * (part + 1)],
+                    in_=bands6[:].rearrange("p n r (c wi) -> p n (r c) wi", wi=4),
+                    axis=AXIS.X,
+                    op=ADD,
+                )
+
+            steps = [add_two, add_third, middle_band, outer_bands, level8, level6]
+            if part == 1:
+                steps += means(b, first, last)
+            return steps
+
+        def means(b, first, last):
+            sums = sums_of[b][:, first:last, :]
+            level6 = sums[:, :, AT6:AT8]
+
+            def level3():
+                for r in range(3):
+                    nc.vector.tensor_reduce(
+                        out=sums[:, :, AT3 + 3 * r : AT3 + 3 * (r + 1)],
+                        in_=level6[:, :, 12 * r : 12 * (r + 1)].rearrange(
+                            "p n (hi c wi) -> p n c hi wi", hi=2, wi=2
+                        ),
+                        axis=AXIS.XY,
+                        op=ADD,
+                    )
+
+            def whole():
+                nc.vector.tensor_reduce(out=sums[:, :, 0:AT3], in_=level6, axis=AXIS.X, op=ADD)
+
+            def key_means():
+                keys = max(first, 1)
+                tok = sums_pool.tile([P, last - keys, TOKENS], F32, name="tok")
+                nc.vector.tensor_tensor(
+                    out=tok[:],
+                    in0=sums_of[b][:, keys:last, :],
+                    in1=inv_area[:].unsqueeze(1).to_broadcast([P, last - keys, TOKENS]),
+                    op=MULT,
+                )
+                nc.sync.dma_start(out=keyp_view[b, :, keys - 1 : last - 1, :], in_=tok[:])
+
+            def value_means():
+                tok = sums_pool.tile([P, P], F32, name="value_tok")
+                nc.vector.memset(tok[:, TOKENS:], 0.0)
+                nc.vector.tensor_tensor(
+                    out=tok[:, 0:TOKENS], in0=sums_of[b][:, 0, :], in1=inv_area[:], op=MULT
+                )
+                tokens_of[b] = tok
+
+            def store_value():
+                turned = psum.tile([P, P], F32, tag="value", bufs=1)
+                nc.tensor.transpose(turned[:], tokens_of[b][:], ident[:])
+                value = sums_pool.tile([P, P], F32, name="value")
+                nc.scalar.copy(out=value[:], in_=turned[:])
+                nc.sync.dma_start(out=out_2[b], in_=value[0:TOKENS, :])
+
+            steps = [level3, whole]
+            if first == 0:
+                steps += [value_means, store_value]
+            return steps + [key_means]
 
         groups = [[VALUE_TILE]] + [[m, m + 1] for m in range(0, KEY_TILES, 2)]
         tile_order = [m for tiles in groups for m in tiles]
@@ -278,8 +357,14 @@ def tile_apnb_pa_t_kernel(
         prepare_weights(tile_order[0])
         quantise_x(0, PASSES - 1)
 
+        due = []
+
+        def work_off(count):
+            for step in due[:count]:
+                step()
+            due[:count] = []
+
         previous = None
-        value_due = None
         for half in range(HALVES):
             following = half + 1
             for step, tiles in enumerate(groups):
@@ -292,18 +377,16 @@ def tile_apnb_pa_t_kernel(
                     quantise_x(following, step // 2 - 1)
 
                 work = {"half": half, "tiles": tiles, "kf": project(half, tiles)}
-                if value_due is not None:
-                    store_value(value_due[0], value_due[1])
-                    value_due = None
 
                 if previous is not None:
                     add_column_pairs(previous)
+                work_off(2)
                 add_row_pairs(work)
-                if previous is not None:
-                    sum_cells(previous)
-                    if previous["half"] % 2 == 1 and previous["tiles"] == groups[-1]:
-                        b = previous["half"] // 2
-                        value_due = (b, finish_image(b))
+                work_off(2)
+                if half > 0 and step == 0:
+                    due.extend(cell_sums(half - 1, 0, TILES))
+                if half == HALVES - 1 and step >= 3:
+                    due.extend(cell_sums(half, *LAST_PARTS[step - 3]))
                 previous = work
 
                 if following < HALVES and step < 2 * PASSES:
@@ -313,5 +396,5 @@ def tile_apnb_pa_t_kernel(
                         regroup_x(following, g, 2, nc.vector.tensor_copy)
 
         add_column_pairs(previous)
-        sum_cells(previous)
-        store_value(IMAGES - 1, finish_image(IMAGES - 1))
+        due.extend(cell_sums(HALVES - 1, *LAST_PARTS[2]))
+        work_off(len(due))

@@ -32,7 +32,6 @@ QUADS = HALF // 4
 TOKENS = 110
 AT3, AT6, AT8 = 1, 10, 46
 EPS = 1e-5
-LAST_PARTS = ((0, 5), (5, 7), (7, 9))
 
 FLOPS = 2 * IMAGES * SIDE * SIDE * 1024 * (1024 + 128)
 
@@ -384,17 +383,24 @@ def tile_apnb_pa_t_kernel(
                 add_row_pairs(work)
                 work_off(2)
                 if half > 0 and step == 0:
-                    due.extend(cell_sums(half - 1, 0, TILES))
-                if half == HALVES - 1 and step >= 3:
-                    due.extend(cell_sums(half, *LAST_PARTS[step - 3]))
+                    due.extend(cell_sums(half - 1, 5, TILES))
+                if step == 3:
+                    due.extend(cell_sums(half, 0, 5))
+                if half == HALVES - 1 and step == 4:
+                    due.extend(cell_sums(half, 5, 7))
                 previous = work
 
                 if following < HALVES and step < 2 * PASSES:
-                    g = step // 2
-                    regroup_x(following, g, step % 2, nc.scalar.copy)
-                    if step % 2 == 1:
-                        regroup_x(following, g, 2, nc.vector.tensor_copy)
+                    g, odd = divmod(step, 2)
+                    if following == 1:
+                        regroup_x(following, g, odd, nc.vector.tensor_copy)
+                        if odd:
+                            regroup_x(following, g, 2, nc.scalar.copy)
+                    else:
+                        regroup_x(following, g, odd, nc.scalar.copy)
+                        if odd:
+                            regroup_x(following, g, 2, nc.vector.tensor_copy)
 
         add_column_pairs(previous)
-        due.extend(cell_sums(HALVES - 1, *LAST_PARTS[2]))
+        due.extend(cell_sums(HALVES - 1, 7, TILES))
         work_off(len(due))

@@ -9,6 +9,7 @@ U32 = mybir.dt.uint32
 U8 = mybir.dt.uint8
 FP8X4 = mybir.dt.float8_e4m3fn_x4
 ACT = mybir.ActivationFunctionType
+ENGINE = mybir.EngineType
 ADD = mybir.AluOpType.add
 MULT = mybir.AluOpType.mult
 AXIS = mybir.AxisListType
@@ -25,7 +26,6 @@ KEY_TILES = 8
 VALUE_TILE = 8
 TILES = KEY_TILES + 1
 BANK = 512
-QUANT_MAX = 4096
 BLOCKS = 3
 BLOCK = HALF // BLOCKS
 QUADS = HALF // 4
@@ -41,14 +41,14 @@ def tile_apnb_pa_t_kernel(
 ):
     nc = tc.nc
 
-    x_view = feats.rearrange("b (g q u e) h w -> b q g u e (h w)", g=PASSES, u=2, e=2)
+    x_view = feats.rearrange("b (g q t) h w -> b q g t (h w)", g=PASSES, t=PACK)
     kf_view = out_0.rearrange("b (p m) h w -> b p m (h w)", m=KEY_TILES)
     keyp_view = out_1.rearrange("b (p m) t -> b p m t", m=KEY_TILES)
 
     with ExitStack() as ctx:
         consts = ctx.enter_context(tc.tile_pool(name="consts", bufs=1))
-        xraw_pool = ctx.enter_context(tc.tile_pool(name="xraw", bufs=3))
-        grouped_pool = ctx.enter_context(tc.tile_pool(name="grouped", bufs=3))
+        xraw_pool = ctx.enter_context(tc.tile_pool(name="xraw", bufs=2))
+        grouped_pool = ctx.enter_context(tc.tile_pool(name="grouped", bufs=2))
         xq_pool = ctx.enter_context(tc.tile_pool(name="xq", bufs=2))
         wstage = ctx.enter_context(tc.tile_pool(name="wstage", bufs=2))
         kf_pool = ctx.enter_context(tc.tile_pool(name="kf", bufs=3))
@@ -58,94 +58,102 @@ def tile_apnb_pa_t_kernel(
         sums_pool = ctx.enter_context(tc.tile_pool(name="sums", bufs=2))
         psum = ctx.enter_context(tc.psum_pool(name="psum", bufs=7))
 
+        warm = consts.tile([P, 1], F32)
+        nc.vector.memset(warm[:], 1.0)
+        nc.scalar.sqrt(out=warm[:], in_=warm[:])
+
         ident = consts.tile([P, P], F32)
         make_identity(nc, ident[:])
 
-        prm = consts.tile([P, 6, 16], BF16)
-        with nc.allow_non_contiguous_dma(reason="8 channels (16 bytes) to a partition"):
-            for slot, vec in enumerate((bk, gk, betak, mk, vk)):
-                nc.scalar.dma_start(
-                    out=prm[:, slot, 0:KEY_TILES],
-                    in_=vec.rearrange("(p m) -> p m", m=KEY_TILES),
-                )
-            nc.scalar.dma_start(out=prm[:, 5, 0:1], in_=bv.rearrange("(p o) -> p o", o=1))
-
         xraw = {}
 
-        def load_x(half, piece, start=0, width=HALF):
-            if half not in xraw:
-                xraw[half] = xraw_pool.tile([P, PASSES, PACK, HALF], BF16, name="xraw")
-            g, u = divmod(piece, 2)
-            first = (half % 2) * HALF
+        def load_x(half, g, start=0, width=HALF):
+            if (half, start) not in xraw:
+                pool = xraw_pool if width == HALF else consts
+                xraw[half, start] = pool.tile([P, PASSES, PACK, width], BF16, name="x_" + str(width))
+            first = (half % 2) * HALF + start
             nc.sync.dma_start(
-                out=xraw[half][:, g, 2 * u : 2 * u + 2, start : start + width],
-                in_=x_view[half // 2, :, g, u, :, first + start : first + start + width],
+                out=xraw[half, start][:, g, :, :],
+                in_=x_view[half // 2, :, g, :, first : first + width],
             )
 
         wv_raw = consts.tile([P, 1024], BF16)
-        for g in range(PASSES):
-            for block in range(BLOCKS):
-                for u in range(2):
-                    load_x(0, 2 * g + u, block * BLOCK, BLOCK)
-            if g == 0:
-                nc.sync.dma_start(out=wv_raw[:], in_=Wv)
         wk_raw = consts.tile([P, KEY_TILES, 1024], BF16)
         wk_view = Wk.rearrange("(p m) k -> p m k", m=KEY_TILES)
-        for m in range(0, KEY_TILES, 2):
+
+        def load_weights(m):
             nc.sync.dma_start(out=wk_raw[:, m : m + 2, :], in_=wk_view[:, m : m + 2, :])
-        for piece in range(4):
-            load_x(1, piece)
+
+        prm = consts.tile([P, 6, 16], BF16)
+
+        def load_vectors():
+            with nc.allow_non_contiguous_dma(reason="8 channels (16 bytes) to a partition"):
+                for slot, vec in enumerate((bk, gk, betak, mk, vk)):
+                    nc.sync.dma_start(
+                        out=prm[:, slot, 0:KEY_TILES],
+                        in_=vec.rearrange("(p m) -> p m", m=KEY_TILES),
+                    )
+                nc.sync.dma_start(out=prm[:, 5, 0:1], in_=bv.rearrange("(p o) -> p o", o=1))
+
+        for g in range(PASSES):
+            load_x(0, g, 0, BANK)
+        nc.sync.dma_start(out=wv_raw[:], in_=Wv)
+        load_vectors()
+        load_weights(0)
+        for g in range(PASSES):
+            load_x(0, g, BANK, HALF - BANK)
+        load_weights(2)
+        load_x(1, 0)
+        load_weights(4)
+        load_x(1, 1)
+        load_weights(6)
 
         scale_t = consts.tile([P, TILES], F32)
         bias_t = consts.tile([P, TILES], F32)
         std = consts.tile([P, KEY_TILES], F32)
-        keys = slice(0, KEY_TILES)
-        nc.vector.tensor_scalar_add(out=std[:], in0=prm[:, 4, keys], scalar1=EPS)
-        nc.scalar.sqrt(out=std[:], in_=std[:])
-        nc.vector.reciprocal(out=std[:], in_=std[:])
-        nc.vector.tensor_mul(out=scale_t[:, keys], in0=std[:], in1=prm[:, 1, keys])
-        nc.vector.tensor_sub(out=bias_t[:, keys], in0=prm[:, 0, keys], in1=prm[:, 3, keys])
-        nc.vector.tensor_mul(out=bias_t[:, keys], in0=bias_t[:, keys], in1=scale_t[:, keys])
-        nc.vector.tensor_add(out=bias_t[:, keys], in0=bias_t[:, keys], in1=prm[:, 2, keys])
-        nc.vector.memset(scale_t[:, VALUE_TILE : VALUE_TILE + 1], 1.0)
-        nc.vector.tensor_copy(out=bias_t[:, VALUE_TILE : VALUE_TILE + 1], in_=prm[:, 5, 0:1])
 
-        ones = consts.tile([P, TOKENS], F32)
-        nc.gpsimd.memset(ones[:], 1.0)
-        inv_area = consts.tile([P, TOKENS], F32)
-        for first, last, side in ((0, AT3, 48), (AT3, AT6, 16), (AT6, AT8, 8), (AT8, TOKENS, 6)):
-            nc.vector.tensor_scalar_mul(
-                out=inv_area[:, first:last], in0=ones[:, first:last], scalar1=1.0 / (side * side)
-            )
+        keys = slice(0, KEY_TILES)
+
+        def begin_norm():
+            nc.vector.tensor_scalar_add(out=std[:], in0=prm[:, 4, keys], scalar1=EPS)
+            nc.vector.tensor_sub(out=bias_t[:, keys], in0=prm[:, 0, keys], in1=prm[:, 3, keys])
+            nc.vector.memset(scale_t[:, VALUE_TILE : VALUE_TILE + 1], 1.0)
+            nc.vector.tensor_copy(out=bias_t[:, VALUE_TILE : VALUE_TILE + 1], in_=prm[:, 5, 0:1])
+            nc.scalar.sqrt(out=std[:], in_=std[:])
+
+        def finish_norm():
+            nc.vector.reciprocal(out=std[:], in_=std[:])
+            nc.vector.tensor_mul(out=scale_t[:, keys], in0=std[:], in1=prm[:, 1, keys])
+            nc.vector.tensor_mul(out=bias_t[:, keys], in0=bias_t[:, keys], in1=scale_t[:, keys])
+            nc.vector.tensor_add(out=bias_t[:, keys], in0=bias_t[:, keys], in1=prm[:, 2, keys])
 
         grouped = {}
         x_codes = {}
         x_scales = {}
 
-        def regroup_x(half, g, block, copy):
-            if block == 0:
+        def regroup_x(half, g, start, width, copy, loaded=0):
+            if start == 0:
                 grouped[half, g] = grouped_pool.tile(
                     [P, HALF, PACK], BF16, name="grouped", align_bytes=64
                 )
-            cols = slice(block * BLOCK, (block + 1) * BLOCK)
+            cols = slice(start, start + width)
             copy(
                 out=grouped[half, g][:, cols, :].rearrange("p (c i) t -> p c t i", i=4),
-                in_=xraw[half][:, g, :, cols].rearrange("p t (c i) -> p c t i", i=4),
+                in_=xraw[half, loaded][:, g, :, start - loaded : start - loaded + width].rearrange("p t (c i) -> p c t i", i=4),
             )
 
-        def quantise_x(half, g):
-            if g == 0:
+        def quantise_x(half, g, widths, start=0):
+            if start == 0 and g == 0:
                 x_codes[half] = xq_pool.tile([P, PASSES, HALF], U32, name="x_codes", align_bytes=64)
                 x_scales[half] = xq_pool.tile([P, PASSES, HALF], U8, name="x_scales", align_bytes=64)
-            flat = grouped[half, g][:].rearrange("p n t -> p (n t)")
-            for first in range(0, HALF * PACK, QUANT_MAX):
-                width = min(QUANT_MAX, HALF * PACK - first)
-                words = slice(first // PACK, (first + width) // PACK)
+            for width in widths:
+                words = slice(start, start + width)
                 nc.vector.quantize_mx(
                     out=x_codes[half][:, g, words].bitcast(FP8X4),
                     scales=x_scales[half][:, g, words],
-                    in_=flat[:, first : first + width],
+                    in_=grouped[half, g][:, words, :].rearrange("p n t -> p (n t)"),
                 )
+                start += width
 
         w_codes = consts.tile([P, TILES, PASSES * P], U32, align_bytes=64)
         w_scales = consts.tile([P, TILES, PASSES * P], U8, align_bytes=64)
@@ -172,36 +180,41 @@ def tile_apnb_pa_t_kernel(
                 in_=w_grouped[:].rearrange("q g c t -> q (g c t)"),
             )
 
-        def project(half, tiles):
+        def open_step(half, tiles):
             kf = kf_pool.tile([P, len(tiles), HALF], F32, name="kf")
-            for j, m in enumerate(tiles):
-                for first in range(0, HALF, BANK):
-                    width = min(BANK, HALF - first)
-                    acc = psum.tile([P, BANK], F32, tag="acc")
-                    for g in range(PASSES):
-                        nc.tensor.matmul_mx(
-                            out=acc[:, 0:width],
-                            lhsT=w_codes[:, m, g * P : (g + 1) * P].bitcast(FP8X4),
-                            lhsT_scale=w_scales[:, m, g * P : (g + 1) * P],
-                            rhs=x_codes[half][:, g, first : first + width].bitcast(FP8X4),
-                            rhs_scale=x_scales[half][:, g, first : first + width],
-                            start=(g == 0),
-                            stop=(g == PASSES - 1),
-                        )
-                    nc.scalar.activation(
-                        out=kf[:, j, first : first + width],
-                        in_=acc[:, 0:width],
-                        func=ACT.Identity if m == VALUE_TILE else ACT.Relu,
-                        bias=bias_t[:, m : m + 1],
-                        scale=scale_t[:, m : m + 1],
+            return {"half": half, "tiles": tiles, "kf": kf}
+
+        def project(work, first, width):
+            half = work["half"]
+            for j, m in enumerate(work["tiles"]):
+                acc = psum.tile([P, BANK], F32, tag="acc")
+                for g in range(PASSES):
+                    nc.tensor.matmul_mx(
+                        out=acc[:, 0:width],
+                        lhsT=w_codes[:, m, g * P : (g + 1) * P].bitcast(FP8X4),
+                        lhsT_scale=w_scales[:, m, g * P : (g + 1) * P],
+                        rhs=x_codes[half][:, g, first : first + width].bitcast(FP8X4),
+                        rhs_scale=x_scales[half][:, g, first : first + width],
+                        start=(g == 0),
+                        stop=(g == PASSES - 1),
                     )
-            if tiles[0] != VALUE_TILE:
-                first = (half % 2) * HALF
-                nc.sync.dma_start(
-                    out=kf_view[half // 2, :, tiles[0] : tiles[0] + len(tiles), first : first + HALF],
-                    in_=kf[:],
+                nc.scalar.activation(
+                    out=work["kf"][:, j, first : first + width],
+                    in_=acc[:, 0:width],
+                    func=ACT.Identity if m == VALUE_TILE else ACT.Relu,
+                    bias=bias_t[:, m : m + 1],
+                    scale=scale_t[:, m : m + 1],
                 )
-            return kf
+
+        def store_keys(work):
+            half = work["half"]
+            first = (half % 2) * HALF
+            keys = [m for m in work["tiles"] if m != VALUE_TILE]
+            skip = len(work["tiles"]) - len(keys)
+            nc.sync.dma_start(
+                out=kf_view[half // 2, :, keys[0] : keys[-1] + 1, first : first + HALF],
+                in_=work["kf"][:, skip:, :],
+            )
 
         def slot_of(m):
             return 0 if m == VALUE_TILE else m + 1
@@ -344,17 +357,37 @@ def tile_apnb_pa_t_kernel(
                 steps += [value_means, store_value]
             return steps + [key_means]
 
-        groups = [[VALUE_TILE]] + [[m, m + 1] for m in range(0, KEY_TILES, 2)]
-        tile_order = [m for tiles in groups for m in tiles]
+        groups = [[VALUE_TILE, 0, 1]] + [[m, m + 1] for m in range(2, KEY_TILES, 2)]
 
-        for g in range(PASSES):
-            regroup_x(0, g, 0, nc.vector.tensor_copy)
-            regroup_x(0, g, 1, nc.vector.tensor_copy)
-            regroup_x(0, g, 2, nc.scalar.copy)
-            if g > 0:
-                quantise_x(0, g - 1)
-        prepare_weights(tile_order[0])
-        quantise_x(0, PASSES - 1)
+        with tc.manual_schedule(engines={ENGINE.PE, ENGINE.Activation, ENGINE.DVE}):
+            first_step = open_step(0, groups[0])
+            share = 320
+            regroup_x(0, 0, 0, share, nc.vector.tensor_copy)
+            regroup_x(0, 0, share, BANK - share, nc.scalar.copy)
+            quantise_x(0, 0, (BANK,))
+            regroup_x(0, 1, 0, share, nc.vector.tensor_copy)
+            regroup_x(0, 1, share, BANK - share, nc.scalar.copy)
+            begin_norm()
+            prepare_weights(VALUE_TILE)
+            quantise_x(0, 1, (BANK,))
+            finish_norm()
+            for m in groups[0][1:]:
+                prepare_weights(m)
+            project(first_step, 0, BANK)
+            share = 448
+            for g in range(PASSES):
+                regroup_x(0, g, BANK, share, nc.vector.tensor_copy, BANK)
+                regroup_x(0, g, BANK + share, HALF - BANK - share, nc.scalar.copy, BANK)
+            for g in range(PASSES):
+                quantise_x(0, g, (BANK, HALF - 2 * BANK), BANK)
+
+        ones = consts.tile([P, TOKENS], F32)
+        nc.gpsimd.memset(ones[:], 1.0)
+        inv_area = consts.tile([P, TOKENS], F32)
+        for first, last, side in ((0, AT3, 48), (AT3, AT6, 16), (AT6, AT8, 8), (AT8, TOKENS, 6)):
+            nc.vector.tensor_scalar_mul(
+                out=inv_area[:, first:last], in0=ones[:, first:last], scalar1=1.0 / (side * side)
+            )
 
         due = []
 
@@ -363,6 +396,8 @@ def tile_apnb_pa_t_kernel(
                 step()
             due[:count] = []
 
+        blocks_of = (((0, 0), (0, 1)), ((0, 2), (1, 0)), ((1, 1), (1, 2)), ())
+
         previous = None
         for half in range(HALVES):
             following = half + 1
@@ -370,36 +405,42 @@ def tile_apnb_pa_t_kernel(
                 if half == 0 and step + 1 < len(groups):
                     for m in groups[step + 1]:
                         prepare_weights(m)
-                if half + 2 < HALVES and step < 4:
+                if half + 2 < HALVES and step < PASSES:
                     load_x(half + 2, step)
-                if following < HALVES and step >= 2 and step % 2 == 0:
-                    quantise_x(following, step // 2 - 1)
+                if following < HALVES and step >= 2:
+                    quantise_x(following, step - 2, (2 * BANK, HALF - 2 * BANK))
 
-                work = {"half": half, "tiles": tiles, "kf": project(half, tiles)}
+                if half == 0 and step == 0:
+                    work, begun = first_step, BANK
+                else:
+                    work, begun = open_step(half, tiles), 0
+                for first in range(begun, HALF, BANK):
+                    project(work, first, min(BANK, HALF - first))
+                store_keys(work)
 
                 if previous is not None:
                     add_column_pairs(previous)
-                work_off(2)
+                work_off(3)
                 add_row_pairs(work)
-                work_off(2)
+                work_off(3)
                 if half > 0 and step == 0:
                     due.extend(cell_sums(half - 1, 5, TILES))
-                if step == 3:
+                if step == 2:
                     due.extend(cell_sums(half, 0, 5))
-                if half == HALVES - 1 and step == 4:
+                if half == HALVES - 1 and step == 3:
                     due.extend(cell_sums(half, 5, 7))
                 previous = work
 
-                if following < HALVES and step < 2 * PASSES:
-                    g, odd = divmod(step, 2)
-                    if following == 1:
-                        regroup_x(following, g, odd, nc.vector.tensor_copy)
-                        if odd:
-                            regroup_x(following, g, 2, nc.scalar.copy)
-                    else:
-                        regroup_x(following, g, odd, nc.scalar.copy)
-                        if odd:
-                            regroup_x(following, g, 2, nc.vector.tensor_copy)
+                if following < HALVES:
+                    for g, block in blocks_of[step]:
+                        on_vector = block < 2 if following == 1 else block == 2
+                        regroup_x(
+                            following,
+                            g,
+                            block * BLOCK,
+                            BLOCK,
+                            nc.vector.tensor_copy if on_vector else nc.scalar.copy,
+                        )
 
         add_column_pairs(previous)
         due.extend(cell_sums(HALVES - 1, 7, TILES))

@@ -182,7 +182,10 @@ def tile_apnb_pa_t_kernel(
 
         def open_step(half, tiles):
             kf = kf_pool.tile([P, len(tiles), HALF], F32, name="kf")
-            return {"half": half, "tiles": tiles, "kf": kf}
+            on_tensor = [0] if tiles[0] == VALUE_TILE else []
+            if half == HALVES - 1 and tiles[-1] == KEY_TILES - 1:
+                on_tensor = [len(tiles) - 1]
+            return {"half": half, "tiles": tiles, "kf": kf, "on_tensor": on_tensor}
 
         def project(work, first, width):
             half = work["half"]
@@ -223,22 +226,51 @@ def tile_apnb_pa_t_kernel(
         sums_of = {}
         tokens_of = {}
 
+        def quads_tile(half):
+            if half not in quads_of:
+                quads_of[half] = quads_pool.tile([P, TILES, QUADS], F32, name="quads")
+            return quads_of[half]
+
+        def sum_quads(work, j):
+            pixels = work["kf"][:, j, :].rearrange("p (a r c d) -> p r d a c", r=2, c=24, d=2)
+            acc = psum.tile([P, BANK], F32, tag="acc")
+            for corner in range(4):
+                nc.tensor.matmul(
+                    acc[:, 0:QUADS].rearrange("p (a c) -> p a c", c=24),
+                    lhsT=ident[:],
+                    rhs=pixels[:, corner // 2, corner % 2],
+                    start=(corner == 0),
+                    stop=(corner == 3),
+                )
+            work["quads_acc"] = acc
+
+        def take_quads(work, j):
+            slot = slot_of(work["tiles"][j])
+            nc.scalar.copy(
+                out=quads_tile(work["half"])[:, slot, :], in_=work["quads_acc"][:, 0:QUADS]
+            )
+
+        def vector_tiles(work):
+            count = len(work["tiles"])
+            if work["tiles"][0] == VALUE_TILE:
+                return 1, count
+            return 0, count - len(work["on_tensor"])
+
         def add_row_pairs(work):
-            kf = work["kf"]
-            pairs = pool_tmp.tile([P, len(work["tiles"]) * HALF_ROWS // 2, SIDE], F32, name="row_pairs")
-            rows = kf[:].rearrange("p n (a two w) -> p (n a) two w", two=2, w=SIDE)
+            begin, end = vector_tiles(work)
+            kf = work["kf"][:, begin:end, :]
+            pairs = pool_tmp.tile([P, (end - begin) * HALF_ROWS // 2, SIDE], F32, name="row_pairs")
+            rows = kf.rearrange("p n (a two w) -> p (n a) two w", two=2, w=SIDE)
             nc.vector.tensor_tensor(out=pairs[:], in0=rows[:, :, 0, :], in1=rows[:, :, 1, :], op=ADD)
             work["row_pairs"] = pairs
 
         def add_column_pairs(work):
-            half, tiles, pairs = work["half"], work["tiles"], work["row_pairs"]
-            if half not in quads_of:
-                quads_of[half] = quads_pool.tile([P, TILES, QUADS], F32, name="quads")
+            begin, end = vector_tiles(work)
+            pairs = work["row_pairs"]
             cols = pairs[:].rearrange("p a (c two) -> p (a c) two", two=2)
-            slot = slot_of(tiles[0])
-            span = slice(slot, slot + len(tiles))
+            slot = slot_of(work["tiles"][begin])
             nc.vector.tensor_tensor(
-                out=quads_of[half][:, span, :].rearrange("p n q -> p (n q)"),
+                out=quads_tile(work["half"])[:, slot : slot + end - begin, :].rearrange("p n q -> p (n q)"),
                 in0=cols[:, :, 0],
                 in1=cols[:, :, 1],
                 op=ADD,
@@ -401,6 +433,7 @@ def tile_apnb_pa_t_kernel(
         previous = None
         for half in range(HALVES):
             following = half + 1
+            burst = 3 if following < HALVES else 12
             for step, tiles in enumerate(groups):
                 if half == 0 and step + 1 < len(groups):
                     for m in groups[step + 1]:
@@ -416,13 +449,19 @@ def tile_apnb_pa_t_kernel(
                     work, begun = open_step(half, tiles), 0
                 for first in range(begun, HALF, BANK):
                     project(work, first, min(BANK, HALF - first))
+                    if previous is not None:
+                        for j in previous["on_tensor"]:
+                            if first == 0:
+                                sum_quads(previous, j)
+                            elif first == BANK:
+                                take_quads(previous, j)
                 store_keys(work)
 
                 if previous is not None:
                     add_column_pairs(previous)
-                work_off(3)
+                work_off(burst)
                 add_row_pairs(work)
-                work_off(3)
+                work_off(burst)
                 if half > 0 and step == 0:
                     due.extend(cell_sums(half - 1, 5, TILES))
                 if step == 2:
@@ -442,6 +481,9 @@ def tile_apnb_pa_t_kernel(
                             nc.vector.tensor_copy if on_vector else nc.scalar.copy,
                         )
 
+        for j in previous["on_tensor"]:
+            sum_quads(previous, j)
+            take_quads(previous, j)
         add_column_pairs(previous)
         due.extend(cell_sums(HALVES - 1, 7, TILES))
         work_off(len(due))

@@ -32,6 +32,11 @@ QUADS = HALF // 4
 TOKENS = 110
 AT3, AT6, AT8 = 1, 10, 46
 EPS = 1e-5
+VECTOR_BLOCKS = {
+    1: ((0, 0), (0, 1), (0, 2), (1, 0), (1, 2)),
+    2: ((0, 1), (1, 0), (1, 2)),
+    3: ((0, 1), (1, 0), (1, 2)),
+}
 
 FLOPS = 2 * IMAGES * SIDE * SIDE * 1024 * (1024 + 128)
 
@@ -472,7 +477,7 @@ def tile_apnb_pa_t_kernel(
 
                 if following < HALVES:
                     for g, block in blocks_of[step]:
-                        on_vector = block < 2 if following == 1 else block == 2
+                        on_vector = (g, block) in VECTOR_BLOCKS[following]
                         regroup_x(
                             following,
                             g,

@@ -454,13 +454,12 @@ def tile_apnb_pa_t_kernel(
                     work, begun = open_step(half, tiles), 0
                 for first in range(begun, HALF, BANK):
                     project(work, first, min(BANK, HALF - first))
-                    if previous is not None:
-                        for j in previous["on_tensor"]:
-                            if first == 0:
-                                sum_quads(previous, j)
-                            elif first == BANK:
-                                take_quads(previous, j)
                 store_keys(work)
+
+                if previous is not None and following == HALVES:
+                    for j in previous["on_tensor"]:
+                        sum_quads(previous, j)
+                        take_quads(previous, j)
 
                 if previous is not None:
                     add_column_pairs(previous)
@@ -473,7 +472,7 @@ def tile_apnb_pa_t_kernel(
                     due.extend(cell_sums(half, 0, 5))
                 if half == HALVES - 1 and step == 3:
                     due.extend(cell_sums(half, 5, 7))
-                previous = work
+                finished, previous = previous, work
 
                 if following < HALVES:
                     for g, block in blocks_of[step]:
@@ -485,6 +484,10 @@ def tile_apnb_pa_t_kernel(
                             BLOCK,
                             nc.vector.tensor_copy if on_vector else nc.scalar.copy,
                         )
+                    if finished is not None:
+                        for j in finished["on_tensor"]:
+                            sum_quads(finished, j)
+                            take_quads(finished, j)
 
         for j in previous["on_tensor"]:
             sum_quads(previous, j)

@@ -12,6 +12,7 @@ ACT = mybir.ActivationFunctionType
 ENGINE = mybir.EngineType
 ADD = mybir.AluOpType.add
 MULT = mybir.AluOpType.mult
+SUBTRACT = mybir.AluOpType.subtract
 AXIS = mybir.AxisListType
 
 P = 128
@@ -65,7 +66,7 @@ def tile_apnb_pa_t_kernel(
 
         warm = consts.tile([P, 1], F32)
         nc.vector.memset(warm[:], 1.0)
-        nc.scalar.sqrt(out=warm[:], in_=warm[:])
+        nc.scalar.activation(out=warm[:], in_=warm[:], func=ACT.Abs_reciprocal_sqrt)
 
         ident = consts.tile([P, P], F32)
         make_identity(nc, ident[:])
@@ -103,10 +104,10 @@ def tile_apnb_pa_t_kernel(
         for g in range(PASSES):
             load_x(0, g, 0, BANK)
         nc.sync.dma_start(out=wv_raw[:], in_=Wv)
-        load_vectors()
-        load_weights(0)
         for g in range(PASSES):
             load_x(0, g, BANK, HALF - BANK)
+        load_weights(0)
+        load_vectors()
         load_weights(2)
         load_x(1, 0)
         load_weights(4)
@@ -115,22 +116,20 @@ def tile_apnb_pa_t_kernel(
 
         scale_t = consts.tile([P, TILES], F32)
         bias_t = consts.tile([P, TILES], F32)
-        std = consts.tile([P, KEY_TILES], F32)
+        rstd = consts.tile([P, KEY_TILES], F32)
 
         keys = slice(0, KEY_TILES)
 
-        def begin_norm():
-            nc.vector.tensor_scalar_add(out=std[:], in0=prm[:, 4, keys], scalar1=EPS)
-            nc.vector.tensor_sub(out=bias_t[:, keys], in0=prm[:, 0, keys], in1=prm[:, 3, keys])
-            nc.vector.memset(scale_t[:, VALUE_TILE : VALUE_TILE + 1], 1.0)
-            nc.vector.tensor_copy(out=bias_t[:, VALUE_TILE : VALUE_TILE + 1], in_=prm[:, 5, 0:1])
-            nc.scalar.sqrt(out=std[:], in_=std[:])
+        nc.gpsimd.memset(scale_t[:, VALUE_TILE : VALUE_TILE + 1], 1.0)
 
-        def finish_norm():
-            nc.vector.reciprocal(out=std[:], in_=std[:])
-            nc.vector.tensor_mul(out=scale_t[:, keys], in0=std[:], in1=prm[:, 1, keys])
-            nc.vector.tensor_mul(out=bias_t[:, keys], in0=bias_t[:, keys], in1=scale_t[:, keys])
-            nc.vector.tensor_add(out=bias_t[:, keys], in0=bias_t[:, keys], in1=prm[:, 2, keys])
+        def fold_norm():
+            nc.gpsimd.tensor_scalar_add(out=rstd[:], in0=prm[:, 4, keys], scalar1=EPS)
+            nc.scalar.activation(out=rstd[:], in_=rstd[:], func=ACT.Abs_reciprocal_sqrt)
+            nc.gpsimd.tensor_copy(out=bias_t[:, VALUE_TILE : VALUE_TILE + 1], in_=prm[:, 5, 0:1])
+            nc.gpsimd.tensor_tensor(out=bias_t[:, keys], in0=prm[:, 0, keys], in1=prm[:, 3, keys], op=SUBTRACT)
+            nc.gpsimd.tensor_tensor(out=scale_t[:, keys], in0=rstd[:], in1=prm[:, 1, keys], op=MULT)
+            nc.gpsimd.tensor_tensor(out=bias_t[:, keys], in0=bias_t[:, keys], in1=scale_t[:, keys], op=MULT)
+            nc.gpsimd.tensor_tensor(out=bias_t[:, keys], in0=bias_t[:, keys], in1=prm[:, 2, keys], op=ADD)
 
         grouped = {}
         x_codes = {}
@@ -163,7 +162,9 @@ def tile_apnb_pa_t_kernel(
         w_codes = consts.tile([P, TILES, PASSES * P], U32, align_bytes=64)
         w_scales = consts.tile([P, TILES, PASSES * P], U8, align_bytes=64)
 
-        def prepare_weights(m):
+        w_grouped = {}
+
+        def turn_weights(m):
             rows = wv_raw[:] if m == VALUE_TILE else wk_raw[:, m, :]
             words = rows.bitcast(F32)
             turned = psum.tile([P, BANK], F32, tag="acc")
@@ -174,15 +175,17 @@ def tile_apnb_pa_t_kernel(
                     words[:, g * 2 * P + u : (g + 1) * 2 * P : 2],
                     ident[:],
                 )
-            w_grouped = wstage.tile([P, PASSES, P, PACK], BF16, align_bytes=64)
+            w_grouped[m] = wstage.tile([P, PASSES, P, PACK], BF16, name="w_grouped", align_bytes=64)
             nc.scalar.copy(
-                out=w_grouped[:].bitcast(F32),
+                out=w_grouped[m][:].bitcast(F32),
                 in_=turned[:].rearrange("q (g u c) -> q g c u", g=PASSES, u=2),
             )
+
+        def quantise_weights(m):
             nc.vector.quantize_mx(
                 out=w_codes[:, m, :].bitcast(FP8X4),
                 scales=w_scales[:, m, :],
-                in_=w_grouped[:].rearrange("q g c t -> q (g c t)"),
+                in_=w_grouped[m][:].rearrange("q g c t -> q (g c t)"),
             )
 
         def open_step(half, tiles):
@@ -397,32 +400,29 @@ def tile_apnb_pa_t_kernel(
         groups = [[VALUE_TILE, 0, 1]] + [[m, m + 1] for m in range(2, KEY_TILES, 2)]
 
         with tc.manual_schedule(engines={ENGINE.PE, ENGINE.Activation, ENGINE.DVE}):
-            first_step = open_step(0, groups[0])
-            share = 320
-            regroup_x(0, 0, 0, share, nc.vector.tensor_copy)
-            regroup_x(0, 0, share, BANK - share, nc.scalar.copy)
-            quantise_x(0, 0, (BANK,))
-            regroup_x(0, 1, 0, share, nc.vector.tensor_copy)
-            regroup_x(0, 1, share, BANK - share, nc.scalar.copy)
-            begin_norm()
-            prepare_weights(VALUE_TILE)
-            quantise_x(0, 1, (BANK,))
-            finish_norm()
+            near = 320
+            far = 320
+            for g in range(PASSES):
+                regroup_x(0, g, 0, near, nc.vector.tensor_copy)
+                regroup_x(0, g, near, BANK - near, nc.scalar.copy)
+            for g in range(PASSES):
+                quantise_x(0, g, (BANK,))
+                regroup_x(0, g, BANK, far, nc.vector.tensor_copy, BANK)
+                regroup_x(0, g, BANK + far, HALF - BANK - far, nc.scalar.copy, BANK)
+                if g == 0:
+                    turn_weights(VALUE_TILE)
+            fold_norm()
+            quantise_weights(VALUE_TILE)
             for m in groups[0][1:]:
-                prepare_weights(m)
-            project(first_step, 0, BANK)
-            share = 448
-            for g in range(PASSES):
-                regroup_x(0, g, BANK, share, nc.vector.tensor_copy, BANK)
-                regroup_x(0, g, BANK + share, HALF - BANK - share, nc.scalar.copy, BANK)
-            for g in range(PASSES):
-                quantise_x(0, g, (BANK, HALF - 2 * BANK), BANK)
+                turn_weights(m)
+                quantise_x(0, m, (BANK, HALF - 2 * BANK), BANK)
+                quantise_weights(m)
 
         ones = consts.tile([P, TOKENS], F32)
         nc.gpsimd.memset(ones[:], 1.0)
         inv_area = consts.tile([P, TOKENS], F32)
         for first, last, side in ((0, AT3, 48), (AT3, AT6, 16), (AT6, AT8, 8), (AT8, TOKENS, 6)):
-            nc.vector.tensor_scalar_mul(
+            nc.gpsimd.tensor_scalar_mul(
                 out=inv_area[:, first:last], in0=ones[:, first:last], scalar1=1.0 / (side * side)
             )
 
@@ -442,17 +442,15 @@ def tile_apnb_pa_t_kernel(
             for step, tiles in enumerate(groups):
                 if half == 0 and step + 1 < len(groups):
                     for m in groups[step + 1]:
-                        prepare_weights(m)
+                        turn_weights(m)
+                        quantise_weights(m)
                 if half + 2 < HALVES and step < PASSES:
                     load_x(half + 2, step)
                 if following < HALVES and step >= 2:
                     quantise_x(following, step - 2, (2 * BANK, HALF - 2 * BANK))
 
-                if half == 0 and step == 0:
-                    work, begun = first_step, BANK
-                else:
-                    work, begun = open_step(half, tiles), 0
-                for first in range(begun, HALF, BANK):
+                work = open_step(half, tiles)
+                for first in range(0, HALF, BANK):
                     project(work, first, min(BANK, HALF - first))
                 store_keys(work)
 

@@ -106,8 +106,8 @@ def tile_apnb_pa_t_kernel(
         nc.sync.dma_start(out=wv_raw[:], in_=Wv)
         for g in range(PASSES):
             load_x(0, g, BANK, HALF - BANK)
-        load_weights(0)
         load_vectors()
+        load_weights(0)
         load_weights(2)
         load_x(1, 0)
         load_weights(4)
@@ -123,13 +123,18 @@ def tile_apnb_pa_t_kernel(
         nc.gpsimd.memset(scale_t[:, VALUE_TILE : VALUE_TILE + 1], 1.0)
 
         def fold_norm():
-            nc.gpsimd.tensor_scalar_add(out=rstd[:], in0=prm[:, 4, keys], scalar1=EPS)
-            nc.scalar.activation(out=rstd[:], in_=rstd[:], func=ACT.Abs_reciprocal_sqrt)
-            nc.gpsimd.tensor_copy(out=bias_t[:, VALUE_TILE : VALUE_TILE + 1], in_=prm[:, 5, 0:1])
-            nc.gpsimd.tensor_tensor(out=bias_t[:, keys], in0=prm[:, 0, keys], in1=prm[:, 3, keys], op=SUBTRACT)
-            nc.gpsimd.tensor_tensor(out=scale_t[:, keys], in0=rstd[:], in1=prm[:, 1, keys], op=MULT)
-            nc.gpsimd.tensor_tensor(out=bias_t[:, keys], in0=bias_t[:, keys], in1=scale_t[:, keys], op=MULT)
-            nc.gpsimd.tensor_tensor(out=bias_t[:, keys], in0=bias_t[:, keys], in1=prm[:, 2, keys], op=ADD)
+            nc.scalar.activation(
+                out=rstd[:], in_=prm[:, 4, keys], func=ACT.Abs_reciprocal_sqrt, bias=EPS
+            )
+            nc.scalar.copy(out=bias_t[:, VALUE_TILE : VALUE_TILE + 1], in_=prm[:, 5, 0:1])
+            nc.vector.tensor_tensor(out=bias_t[:, keys], in0=prm[:, 0, keys], in1=prm[:, 3, keys], op=SUBTRACT)
+            nc.vector.tensor_tensor(out=scale_t[:, keys], in0=rstd[:], in1=prm[:, 1, keys], op=MULT)
+
+        def finish_norm():
+            nc.vector.tensor_tensor(out=bias_t[:, keys], in0=bias_t[:, keys], in1=scale_t[:, keys], op=MULT)
+
+        def finish_bias():
+            nc.vector.tensor_tensor(out=bias_t[:, keys], in0=bias_t[:, keys], in1=prm[:, 2, keys], op=ADD)
 
         grouped = {}
         x_codes = {}
@@ -413,9 +418,12 @@ def tile_apnb_pa_t_kernel(
                     turn_weights(VALUE_TILE)
             fold_norm()
             quantise_weights(VALUE_TILE)
+            finish_norm()
             for m in groups[0][1:]:
                 turn_weights(m)
                 quantise_x(0, m, (BANK, HALF - 2 * BANK), BANK)
+                if m == 0:
+                    finish_bias()
                 quantise_weights(m)
 
         ones = consts.tile([P, TOKENS], F32)

@@ -32,12 +32,15 @@ BLOCK = HALF // BLOCKS
 QUADS = HALF // 4
 TOKENS = 110
 AT3, AT6, AT8 = 1, 10, 46
+SIDES = (1, 3, 6, 8)
 EPS = 1e-5
 VECTOR_BLOCKS = {
     1: ((0, 0), (0, 1), (0, 2), (1, 0), (1, 2)),
     2: ((0, 1), (1, 0), (1, 2)),
     3: ((0, 1), (1, 0), (1, 2)),
 }
+
+TENSOR_TILES = ((1, 3), (2, 3))
 
 FLOPS = 2 * IMAGES * SIDE * SIDE * 1024 * (1024 + 128)
 
@@ -57,7 +60,8 @@ def tile_apnb_pa_t_kernel(
         grouped_pool = ctx.enter_context(tc.tile_pool(name="grouped", bufs=2))
         xq_pool = ctx.enter_context(tc.tile_pool(name="xq", bufs=2))
         wstage = ctx.enter_context(tc.tile_pool(name="wstage", bufs=2))
-        kf_pool = ctx.enter_context(tc.tile_pool(name="kf", bufs=3))
+        kf_pool = ctx.enter_context(tc.tile_pool(name="kf", bufs=4))
+        value_pool = ctx.enter_context(tc.tile_pool(name="value_map", bufs=2))
         pool_tmp = ctx.enter_context(tc.tile_pool(name="pool_tmp", bufs=2))
         quads_pool = ctx.enter_context(tc.tile_pool(name="quads", bufs=2))
         band_pool = ctx.enter_context(tc.tile_pool(name="bands", bufs=1))
@@ -194,11 +198,16 @@ def tile_apnb_pa_t_kernel(
             )
 
         def open_step(half, tiles):
-            kf = kf_pool.tile([P, len(tiles), HALF], F32, name="kf")
+            keys = [m for m in tiles if m != VALUE_TILE]
+            kf = kf_pool.tile([P, len(keys), HALF], F32, name="kf")
+            maps = [kf[:, i, :] for i in range(len(keys))]
+            if len(keys) < len(tiles):
+                value_map = value_pool.tile([P, HALF], F32, name="value_map")
+                maps = [value_map[:]] + maps
             on_tensor = [0] if tiles[0] == VALUE_TILE else []
-            if half == HALVES - 1 and tiles[-1] == KEY_TILES - 1:
+            if (half, tiles[-1]) in TENSOR_TILES:
                 on_tensor = [len(tiles) - 1]
-            return {"half": half, "tiles": tiles, "kf": kf, "on_tensor": on_tensor}
+            return {"half": half, "tiles": tiles, "kf": kf, "maps": maps, "on_tensor": on_tensor}
 
         def project(work, first, width):
             half = work["half"]
@@ -215,7 +224,7 @@ def tile_apnb_pa_t_kernel(
                         stop=(g == PASSES - 1),
                     )
                 nc.scalar.activation(
-                    out=work["kf"][:, j, first : first + width],
+                    out=work["maps"][j][:, first : first + width],
                     in_=acc[:, 0:width],
                     func=ACT.Identity if m == VALUE_TILE else ACT.Relu,
                     bias=bias_t[:, m : m + 1],
@@ -226,10 +235,9 @@ def tile_apnb_pa_t_kernel(
             half = work["half"]
             first = (half % 2) * HALF
             keys = [m for m in work["tiles"] if m != VALUE_TILE]
-            skip = len(work["tiles"]) - len(keys)
             nc.sync.dma_start(
                 out=kf_view[half // 2, :, keys[0] : keys[-1] + 1, first : first + HALF],
-                in_=work["kf"][:, skip:, :],
+                in_=work["kf"][:],
             )
 
         def slot_of(m):
@@ -237,7 +245,6 @@ def tile_apnb_pa_t_kernel(
 
         quads_of = {}
         sums_of = {}
-        tokens_of = {}
 
         def quads_tile(half):
             if half not in quads_of:
@@ -245,7 +252,7 @@ def tile_apnb_pa_t_kernel(
             return quads_of[half]
 
         def sum_quads(work, j):
-            pixels = work["kf"][:, j, :].rearrange("p (a r c d) -> p r d a c", r=2, c=24, d=2)
+            pixels = work["maps"][j].rearrange("p (a r c d) -> p r d a c", r=2, c=24, d=2)
             acc = psum.tile([P, BANK], F32, tag="acc")
             for corner in range(4):
                 nc.tensor.matmul(
@@ -257,11 +264,18 @@ def tile_apnb_pa_t_kernel(
                 )
             work["quads_acc"] = acc
 
-        def take_quads(work, j):
+        def sum_cells(work, j):
+            b, part = divmod(work["half"], 2)
             slot = slot_of(work["tiles"][j])
-            nc.scalar.copy(
-                out=quads_tile(work["half"])[:, slot, :], in_=work["quads_acc"][:, 0:QUADS]
-            )
+            for sums, bands, size in zip(level_tiles(b)[2:], (3, 4), (4, 3)):
+                nc.vector.tensor_reduce(
+                    out=sums[:, slot, :].rearrange("p (h i c) -> p h i c", h=2, i=bands)[:, part],
+                    in_=work["quads_acc"][:, 0:QUADS].rearrange(
+                        "p (i r c w) -> p i c r w", i=bands, r=size, w=size
+                    ),
+                    axis=AXIS.XY,
+                    op=ADD,
+                )
 
         def vector_tiles(work):
             count = len(work["tiles"])
@@ -271,7 +285,8 @@ def tile_apnb_pa_t_kernel(
 
         def add_row_pairs(work):
             begin, end = vector_tiles(work)
-            kf = work["kf"][:, begin:end, :]
+            skip = 1 if work["tiles"][0] == VALUE_TILE else 0
+            kf = work["kf"][:, begin - skip : end - skip, :]
             pairs = pool_tmp.tile([P, (end - begin) * HALF_ROWS // 2, SIDE], F32, name="row_pairs")
             rows = kf.rearrange("p n (a two w) -> p (n a) two w", two=2, w=SIDE)
             nc.vector.tensor_tensor(out=pairs[:], in0=rows[:, :, 0, :], in1=rows[:, :, 1, :], op=ADD)
@@ -289,15 +304,21 @@ def tile_apnb_pa_t_kernel(
                 op=ADD,
             )
 
+        def level_tiles(b):
+            if b not in sums_of:
+                sums_of[b] = [
+                    sums_pool.tile([P, TILES, side * side], F32, name="level" + str(side))
+                    for side in SIDES
+                ]
+            return sums_of[b]
+
         def cell_sums(half, first, last):
             n = last - first
             b, part = divmod(half, 2)
-            if b not in sums_of:
-                sums_of[b] = sums_pool.tile([P, TILES, TOKENS], F32, name="sums")
             quads = quads_of[half][:, first:last, :]
             sixes = quads.rearrange("p n (i s c) -> p (n i) s c", s=6, c=24)
             rows = quads.rearrange("p n (a c) -> p n a c", c=24)
-            sums = sums_of[b][:, first:last, :]
+            sums6, sums8 = level_tiles(b)[2:]
             two = band_pool.tile([P, n, 4, 24], F32, name="two")
             bands8 = band_pool.tile([P, n, 4, 24], F32, name="bands8")
             bands6 = band_pool.tile([P, n, 3, 24], F32, name="bands6")
@@ -334,7 +355,7 @@ def tile_apnb_pa_t_kernel(
 
             def level8():
                 nc.vector.tensor_reduce(
-                    out=sums[:, :, AT8 + 32 * part : AT8 + 32 * (part + 1)],
+                    out=sums8[:, first:last, 32 * part : 32 * (part + 1)],
                     in_=bands8[:].rearrange("p n r (c wi) -> p n (r c) wi", wi=3),
                     axis=AXIS.X,
                     op=ADD,
@@ -342,67 +363,86 @@ def tile_apnb_pa_t_kernel(
 
             def level6():
                 nc.vector.tensor_reduce(
-                    out=sums[:, :, AT6 + 18 * part : AT6 + 18 * (part + 1)],
+                    out=sums6[:, first:last, 18 * part : 18 * (part + 1)],
                     in_=bands6[:].rearrange("p n r (c wi) -> p n (r c) wi", wi=4),
                     axis=AXIS.X,
                     op=ADD,
                 )
 
-            steps = [add_two, add_third, middle_band, outer_bands, level8, level6]
-            if part == 1:
-                steps += means(b, first, last)
-            return steps
+            return [add_two, add_third, middle_band, outer_bands, level8, level6]
 
-        def means(b, first, last):
-            sums = sums_of[b][:, first:last, :]
-            level6 = sums[:, :, AT6:AT8]
+        def cell_sums_at_once(half, slot):
+            b, part = divmod(half, 2)
 
-            def level3():
-                for r in range(3):
+            def level(sums, bands, size):
+                def reduce():
                     nc.vector.tensor_reduce(
-                        out=sums[:, :, AT3 + 3 * r : AT3 + 3 * (r + 1)],
-                        in_=level6[:, :, 12 * r : 12 * (r + 1)].rearrange(
-                            "p n (hi c wi) -> p n c hi wi", hi=2, wi=2
+                        out=sums[:, slot, :].rearrange("p (h i c) -> p h i c", h=2, i=bands)[:, part],
+                        in_=quads_of[half][:, slot, :].rearrange(
+                            "p (i r c w) -> p i c r w", i=bands, r=size, w=size
                         ),
                         axis=AXIS.XY,
                         op=ADD,
                     )
 
+                return reduce
+
+            sums6, sums8 = level_tiles(b)[2:]
+            return [level(sums6, 3, 4), level(sums8, 4, 3)]
+
+        def means(b, first, last):
+            sums1, sums3, sums6, sums8 = [sums[:, first:last, :] for sums in level_tiles(b)]
+            tok = sums_pool.tile([P, last - first, TOKENS], F32, name="tok")
+
+            def level3():
+                nc.vector.tensor_reduce(
+                    out=sums3.rearrange("p n (r c) -> p (n r) c", c=3),
+                    in_=sums6.rearrange("p n (r hi c wi) -> p (n r) c hi wi", hi=2, c=3, wi=2),
+                    axis=AXIS.XY,
+                    op=ADD,
+                )
+
             def whole():
-                nc.vector.tensor_reduce(out=sums[:, :, 0:AT3], in_=level6, axis=AXIS.X, op=ADD)
+                nc.vector.tensor_reduce(out=sums1, in_=sums6, axis=AXIS.X, op=ADD)
 
-            def key_means():
-                keys = max(first, 1)
-                tok = sums_pool.tile([P, last - keys, TOKENS], F32, name="tok")
-                nc.vector.tensor_tensor(
-                    out=tok[:],
-                    in0=sums_of[b][:, keys:last, :],
-                    in1=inv_area[:].unsqueeze(1).to_broadcast([P, last - keys, TOKENS]),
-                    op=MULT,
-                )
-                nc.sync.dma_start(out=keyp_view[b, :, keys - 1 : last - 1, :], in_=tok[:])
+            def scale(sums, side, at):
+                def multiply():
+                    nc.vector.tensor_scalar_mul(
+                        out=tok[:, :, at : at + side * side],
+                        in0=sums,
+                        scalar1=side * side / (SIDE * SIDE),
+                    )
 
-            def value_means():
-                tok = sums_pool.tile([P, P], F32, name="value_tok")
-                nc.vector.memset(tok[:, TOKENS:], 0.0)
-                nc.vector.tensor_tensor(
-                    out=tok[:, 0:TOKENS], in0=sums_of[b][:, 0, :], in1=inv_area[:], op=MULT
+                return multiply
+
+            def store_keys_means():
+                skip = 1 if first == 0 else 0
+                nc.sync.dma_start(
+                    out=keyp_view[b, :, first + skip - 1 : last - 1, :], in_=tok[:, skip:, :]
                 )
-                tokens_of[b] = tok
 
             def store_value():
                 turned = psum.tile([P, P], F32, tag="value", bufs=1)
-                nc.tensor.transpose(turned[:], tokens_of[b][:], ident[:])
+                flat = tok[:].rearrange("p n t -> p (n t)")
+                nc.tensor.transpose(turned[:], flat[:, 0:P], ident[:])
                 value = sums_pool.tile([P, P], F32, name="value")
                 nc.scalar.copy(out=value[:], in_=turned[:])
                 nc.sync.dma_start(out=out_2[b], in_=value[0:TOKENS, :])
 
-            steps = [level3, whole]
+            steps = [
+                scale(sums8, 8, AT8),
+                level3,
+                whole,
+                scale(sums6, 6, AT6),
+                scale(sums3, 3, AT3),
+                scale(sums1, 1, 0),
+            ]
             if first == 0:
-                steps += [value_means, store_value]
-            return steps + [key_means]
+                steps.append(store_value)
+            return steps + [store_keys_means]
 
         groups = [[VALUE_TILE, 0, 1]] + [[m, m + 1] for m in range(2, KEY_TILES, 2)]
+        last_groups = groups[:-1] + [[m] for m in groups[-1]]
 
         with tc.manual_schedule(engines={ENGINE.PE, ENGINE.Activation, ENGINE.DVE}):
             near = 320
@@ -426,14 +466,6 @@ def tile_apnb_pa_t_kernel(
                     finish_bias()
                 quantise_weights(m)
 
-        ones = consts.tile([P, TOKENS], F32)
-        nc.gpsimd.memset(ones[:], 1.0)
-        inv_area = consts.tile([P, TOKENS], F32)
-        for first, last, side in ((0, AT3, 48), (AT3, AT6, 16), (AT6, AT8, 8), (AT8, TOKENS, 6)):
-            nc.gpsimd.tensor_scalar_mul(
-                out=inv_area[:, first:last], in0=ones[:, first:last], scalar1=1.0 / (side * side)
-            )
-
         due = []
 
         def work_off(count):
@@ -441,21 +473,24 @@ def tile_apnb_pa_t_kernel(
                 step()
             due[:count] = []
 
-        blocks_of = (((0, 0), (0, 1)), ((0, 2), (1, 0)), ((1, 1), (1, 2)), ())
+        blocks_of = tuple(
+            tuple((step, block) for block in range(BLOCKS)) if step < PASSES else ()
+            for step in range(len(groups))
+        )
 
         previous = None
         for half in range(HALVES):
             following = half + 1
             burst = 3 if following < HALVES else 12
-            for step, tiles in enumerate(groups):
+            for step, tiles in enumerate(groups if following < HALVES else last_groups):
                 if half == 0 and step + 1 < len(groups):
                     for m in groups[step + 1]:
                         turn_weights(m)
                         quantise_weights(m)
                 if half + 2 < HALVES and step < PASSES:
                     load_x(half + 2, step)
-                if following < HALVES and step >= 2:
-                    quantise_x(following, step - 2, (2 * BANK, HALF - 2 * BANK))
+                if following < HALVES and 1 <= step <= PASSES:
+                    quantise_x(following, step - 1, (2 * BANK, HALF - 2 * BANK))
 
                 work = open_step(half, tiles)
                 for first in range(0, HALF, BANK):
@@ -465,7 +500,7 @@ def tile_apnb_pa_t_kernel(
                 if previous is not None and following == HALVES:
                     for j in previous["on_tensor"]:
                         sum_quads(previous, j)
-                        take_quads(previous, j)
+                        sum_cells(previous, j)
 
                 if previous is not None:
                     add_column_pairs(previous)
@@ -473,11 +508,17 @@ def tile_apnb_pa_t_kernel(
                 add_row_pairs(work)
                 work_off(burst)
                 if half > 0 and step == 0:
-                    due.extend(cell_sums(half - 1, 5, TILES))
+                    due.extend(cell_sums(half - 1, 5, 8 if (half - 1, 7) in TENSOR_TILES else TILES))
+                    if half == 2:
+                        due.extend(means(0, 0, TILES))
                 if step == 2:
-                    due.extend(cell_sums(half, 0, 5))
+                    due.extend(cell_sums(half, 1, 4 if (half, 3) in TENSOR_TILES else 5))
+                    if half == HALVES - 1:
+                        due.extend(means(1, 0, 5))
                 if half == HALVES - 1 and step == 3:
                     due.extend(cell_sums(half, 5, 7))
+                if half == HALVES - 1 and step == 4:
+                    due.extend(cell_sums_at_once(half, 7))
                 finished, previous = previous, work
 
                 if following < HALVES:
@@ -493,11 +534,9 @@ def tile_apnb_pa_t_kernel(
                     if finished is not None:
                         for j in finished["on_tensor"]:
                             sum_quads(finished, j)
-                            take_quads(finished, j)
+                            sum_cells(finished, j)
 
-        for j in previous["on_tensor"]:
-            sum_quads(previous, j)
-            take_quads(previous, j)
         add_column_pairs(previous)
-        due.extend(cell_sums(HALVES - 1, 7, TILES))
+        due.extend(cell_sums_at_once(HALVES - 1, TILES - 1))
+        due.extend(means(1, 5, TILES))
         work_off(len(due))

@@ -108,10 +108,10 @@ def tile_apnb_pa_t_kernel(
         for g in range(PASSES):
             load_x(0, g, 0, BANK)
         nc.sync.dma_start(out=wv_raw[:], in_=Wv)
+        load_weights(0)
+        load_vectors()
         for g in range(PASSES):
             load_x(0, g, BANK, HALF - BANK)
-        load_vectors()
-        load_weights(0)
         load_weights(2)
         load_x(1, 0)
         load_weights(4)
@@ -253,7 +253,7 @@ def tile_apnb_pa_t_kernel(
 
         def sum_quads(work, j):
             pixels = work["maps"][j].rearrange("p (a r c d) -> p r d a c", r=2, c=24, d=2)
-            acc = psum.tile([P, BANK], F32, tag="acc")
+            acc = psum.tile([P, BANK], F32, tag="spare", bufs=1)
             for corner in range(4):
                 nc.tensor.matmul(
                     acc[:, 0:QUADS].rearrange("p (a c) -> p a c", c=24),
@@ -422,11 +422,11 @@ def tile_apnb_pa_t_kernel(
                 )
 
             def store_value():
-                turned = psum.tile([P, P], F32, tag="value", bufs=1)
+                turned = psum.tile([P, BANK], F32, tag="spare", bufs=1)
                 flat = tok[:].rearrange("p n t -> p (n t)")
-                nc.tensor.transpose(turned[:], flat[:, 0:P], ident[:])
+                nc.tensor.transpose(turned[:, 0:P], flat[:, 0:P], ident[:])
                 value = sums_pool.tile([P, P], F32, name="value")
-                nc.scalar.copy(out=value[:], in_=turned[:])
+                nc.scalar.copy(out=value[:], in_=turned[:, 0:P])
                 nc.sync.dma_start(out=out_2[b], in_=value[0:TOKENS, :])
 
             steps = [
@@ -445,26 +445,29 @@ def tile_apnb_pa_t_kernel(
         last_groups = groups[:-1] + [[m] for m in groups[-1]]
 
         with tc.manual_schedule(engines={ENGINE.PE, ENGINE.Activation, ENGINE.DVE}):
+            first_step = open_step(0, groups[0])
             near = 320
-            far = 320
+            far = 512
             for g in range(PASSES):
                 regroup_x(0, g, 0, near, nc.vector.tensor_copy)
                 regroup_x(0, g, near, BANK - near, nc.scalar.copy)
+            turn_weights(VALUE_TILE)
             for g in range(PASSES):
                 quantise_x(0, g, (BANK,))
-                regroup_x(0, g, BANK, far, nc.vector.tensor_copy, BANK)
-                regroup_x(0, g, BANK + far, HALF - BANK - far, nc.scalar.copy, BANK)
-                if g == 0:
-                    turn_weights(VALUE_TILE)
             fold_norm()
             quantise_weights(VALUE_TILE)
             finish_norm()
             for m in groups[0][1:]:
                 turn_weights(m)
-                quantise_x(0, m, (BANK, HALF - 2 * BANK), BANK)
+                quantise_weights(m)
                 if m == 0:
                     finish_bias()
-                quantise_weights(m)
+            project(first_step, 0, BANK)
+            for g in range(PASSES):
+                regroup_x(0, g, BANK, far, nc.vector.tensor_copy, BANK)
+                regroup_x(0, g, BANK + far, HALF - BANK - far, nc.scalar.copy, BANK)
+            for g in range(PASSES):
+                quantise_x(0, g, (BANK, HALF - 2 * BANK), BANK)
 
         due = []
 
@@ -492,8 +495,11 @@ def tile_apnb_pa_t_kernel(
                 if following < HALVES and 1 <= step <= PASSES:
                     quantise_x(following, step - 1, (2 * BANK, HALF - 2 * BANK))
 
-                work = open_step(half, tiles)
-                for first in range(0, HALF, BANK):
+                if half == 0 and step == 0:
+                    work, begun = first_step, BANK
+                else:
+                    work, begun = open_step(half, tiles), 0
+                for first in range(begun, HALF, BANK):
                     project(work, first, min(BANK, HALF - first))
                 store_keys(work)
 

@@ -35,7 +35,7 @@ AT3, AT6, AT8 = 1, 10, 46
 SIDES = (1, 3, 6, 8)
 EPS = 1e-5
 VECTOR_BLOCKS = {
-    1: ((0, 0), (0, 1), (0, 2), (1, 0), (1, 2)),
+    1: ((0, 0), (0, 1), (1, 0), (1, 2)),
     2: ((0, 1), (1, 0), (1, 2)),
     3: ((0, 1), (1, 0), (1, 2)),
 }

from contextlib import ExitStack

import concourse.mybir as mybir
from concourse.masks import make_identity

F32 = mybir.dt.float32
BF16 = mybir.dt.bfloat16
U32 = mybir.dt.uint32
U8 = mybir.dt.uint8
FP8X4 = mybir.dt.float8_e4m3fn_x4
ACT = mybir.ActivationFunctionType
ENGINE = mybir.EngineType
ADD = mybir.AluOpType.add
MULT = mybir.AluOpType.mult
SUBTRACT = mybir.AluOpType.subtract
AXIS = mybir.AxisListType

P = 128
PACK = 4
PASSES = 2
IMAGES = 2
SIDE = 48
HALF_ROWS = 24
HALF = HALF_ROWS * SIDE
HALVES = 2 * IMAGES
KEY_TILES = 8
VALUE_TILE = 8
TILES = KEY_TILES + 1
BANK = 512
BLOCKS = 3
BLOCK = HALF // BLOCKS
QUADS = HALF // 4
TOKENS = 110
AT3, AT6, AT8 = 1, 10, 46
SIDES = (1, 3, 6, 8)
EPS = 1e-5
VECTOR_BLOCKS = {
    1: ((0, 0), (0, 1), (1, 0), (1, 2)),
    2: ((0, 1), (1, 0), (1, 2)),
    3: ((0, 1), (1, 0), (1, 2)),
}

TENSOR_TILES = ((1, 3), (2, 3))

FLOPS = 2 * IMAGES * SIDE * SIDE * 1024 * (1024 + 128)


def tile_apnb_pa_t_kernel(
    tc, feats, Wk, bk, gk, betak, mk, vk, Wv, bv, out_0, out_1, out_2
):
    nc = tc.nc

    x_view = feats.rearrange("b (g q t) h w -> b q g t (h w)", g=PASSES, t=PACK)
    kf_view = out_0.rearrange("b (p m) h w -> b p m (h w)", m=KEY_TILES)
    keyp_view = out_1.rearrange("b (p m) t -> b p m t", m=KEY_TILES)

    with ExitStack() as ctx:
        consts = ctx.enter_context(tc.tile_pool(name="consts", bufs=1))
        xraw_pool = ctx.enter_context(tc.tile_pool(name="xraw", bufs=2))
        grouped_pool = ctx.enter_context(tc.tile_pool(name="grouped", bufs=2))
        xq_pool = ctx.enter_context(tc.tile_pool(name="xq", bufs=2))
        wstage = ctx.enter_context(tc.tile_pool(name="wstage", bufs=2))
        kf_pool = ctx.enter_context(tc.tile_pool(name="kf", bufs=4))
        value_pool = ctx.enter_context(tc.tile_pool(name="value_map", bufs=2))
        pool_tmp = ctx.enter_context(tc.tile_pool(name="pool_tmp", bufs=2))
        quads_pool = ctx.enter_context(tc.tile_pool(name="quads", bufs=2))
        band_pool = ctx.enter_context(tc.tile_pool(name="bands", bufs=1))
        sums_pool = ctx.enter_context(tc.tile_pool(name="sums", bufs=2))
        psum = ctx.enter_context(tc.psum_pool(name="psum", bufs=7))

        warm = consts.tile([P, 1], F32)
        nc.vector.memset(warm[:], 1.0)
        nc.scalar.activation(out=warm[:], in_=warm[:], func=ACT.Abs_reciprocal_sqrt)

        ident = consts.tile([P, P], F32)
        make_identity(nc, ident[:])

        xraw = {}

        def load_x(half, g, start=0, width=HALF):
            if (half, start) not in xraw:
                pool = xraw_pool if width == HALF else consts
                xraw[half, start] = pool.tile([P, PASSES, PACK, width], BF16, name="x_" + str(width))
            first = (half % 2) * HALF + start
            nc.sync.dma_start(
                out=xraw[half, start][:, g, :, :],
                in_=x_view[half // 2, :, g, :, first : first + width],
            )

        wv_raw = consts.tile([P, 1024], BF16)
        wk_raw = consts.tile([P, KEY_TILES, 1024], BF16)
        wk_view = Wk.rearrange("(p m) k -> p m k", m=KEY_TILES)

        def load_weights(m):
            nc.sync.dma_start(out=wk_raw[:, m : m + 2, :], in_=wk_view[:, m : m + 2, :])

        prm = consts.tile([P, 6, 16], BF16)

        def load_vectors():
            with nc.allow_non_contiguous_dma(reason="8 channels (16 bytes) to a partition"):
                for slot, vec in enumerate((bk, gk, betak, mk, vk)):
                    nc.sync.dma_start(
                        out=prm[:, slot, 0:KEY_TILES],
                        in_=vec.rearrange("(p m) -> p m", m=KEY_TILES),
                    )
                nc.sync.dma_start(out=prm[:, 5, 0:1], in_=bv.rearrange("(p o) -> p o", o=1))

        for g in range(PASSES):
            load_x(0, g, 0, BANK)
        nc.sync.dma_start(out=wv_raw[:], in_=Wv)
        load_weights(0)
        load_vectors()
        for g in range(PASSES):
            load_x(0, g, BANK, HALF - BANK)
        load_weights(2)
        load_x(1, 0)
        load_weights(4)
        load_x(1, 1)
        load_weights(6)

        scale_t = consts.tile([P, TILES], F32)
        bias_t = consts.tile([P, TILES], F32)
        rstd = consts.tile([P, KEY_TILES], F32)

        keys = slice(0, KEY_TILES)

        nc.gpsimd.memset(scale_t[:, VALUE_TILE : VALUE_TILE + 1], 1.0)

        def fold_norm():
            nc.scalar.activation(
                out=rstd[:], in_=prm[:, 4, keys], func=ACT.Abs_reciprocal_sqrt, bias=EPS
            )
            nc.scalar.copy(out=bias_t[:, VALUE_TILE : VALUE_TILE + 1], in_=prm[:, 5, 0:1])
            nc.vector.tensor_tensor(out=bias_t[:, keys], in0=prm[:, 0, keys], in1=prm[:, 3, keys], op=SUBTRACT)
            nc.vector.tensor_tensor(out=scale_t[:, keys], in0=rstd[:], in1=prm[:, 1, keys], op=MULT)

        def finish_norm():
            nc.vector.tensor_tensor(out=bias_t[:, keys], in0=bias_t[:, keys], in1=scale_t[:, keys], op=MULT)

        def finish_bias():
            nc.vector.tensor_tensor(out=bias_t[:, keys], in0=bias_t[:, keys], in1=prm[:, 2, keys], op=ADD)

        grouped = {}
        x_codes = {}
        x_scales = {}

        def regroup_x(half, g, start, width, copy, loaded=0):
            if start == 0:
                grouped[half, g] = grouped_pool.tile(
                    [P, HALF, PACK], BF16, name="grouped", align_bytes=64
                )
            cols = slice(start, start + width)
            copy(
                out=grouped[half, g][:, cols, :].rearrange("p (c i) t -> p c t i", i=4),
                in_=xraw[half, loaded][:, g, :, start - loaded : start - loaded + width].rearrange("p t (c i) -> p c t i", i=4),
            )

        def quantise_x(half, g, widths, start=0):
            if start == 0 and g == 0:
                x_codes[half] = xq_pool.tile([P, PASSES, HALF], U32, name="x_codes", align_bytes=64)
                x_scales[half] = xq_pool.tile([P, PASSES, HALF], U8, name="x_scales", align_bytes=64)
            for width in widths:
                words = slice(start, start + width)
                nc.vector.quantize_mx(
                    out=x_codes[half][:, g, words].bitcast(FP8X4),
                    scales=x_scales[half][:, g, words],
                    in_=grouped[half, g][:, words, :].rearrange("p n t -> p (n t)"),
                )
                start += width

        w_codes = consts.tile([P, TILES, PASSES * P], U32, align_bytes=64)
        w_scales = consts.tile([P, TILES, PASSES * P], U8, align_bytes=64)

        w_grouped = {}

        def turn_weights(m):
            rows = wv_raw[:] if m == VALUE_TILE else wk_raw[:, m, :]
            words = rows.bitcast(F32)
            turned = psum.tile([P, BANK], F32, tag="acc")
            for gu in range(PASSES * 2):
                g, u = divmod(gu, 2)
                nc.tensor.transpose(
                    turned[:, gu * P : (gu + 1) * P],
                    words[:, g * 2 * P + u : (g + 1) * 2 * P : 2],
                    ident[:],
                )
            w_grouped[m] = wstage.tile([P, PASSES, P, PACK], BF16, name="w_grouped", align_bytes=64)
            nc.scalar.copy(
                out=w_grouped[m][:].bitcast(F32),
                in_=turned[:].rearrange("q (g u c) -> q g c u", g=PASSES, u=2),
            )

        def quantise_weights(m):
            nc.vector.quantize_mx(
                out=w_codes[:, m, :].bitcast(FP8X4),
                scales=w_scales[:, m, :],
                in_=w_grouped[m][:].rearrange("q g c t -> q (g c t)"),
            )

        def open_step(half, tiles):
            keys = [m for m in tiles if m != VALUE_TILE]
            kf = kf_pool.tile([P, len(keys), HALF], F32, name="kf")
            maps = [kf[:, i, :] for i in range(len(keys))]
            if len(keys) < len(tiles):
                value_map = value_pool.tile([P, HALF], F32, name="value_map")
                maps = [value_map[:]] + maps
            on_tensor = [0] if tiles[0] == VALUE_TILE else []
            if (half, tiles[-1]) in TENSOR_TILES:
                on_tensor = [len(tiles) - 1]
            return {"half": half, "tiles": tiles, "kf": kf, "maps": maps, "on_tensor": on_tensor}

        def project(work, first, width):
            half = work["half"]
            for j, m in enumerate(work["tiles"]):
                acc = psum.tile([P, BANK], F32, tag="acc")
                for g in range(PASSES):
                    nc.tensor.matmul_mx(
                        out=acc[:, 0:width],
                        lhsT=w_codes[:, m, g * P : (g + 1) * P].bitcast(FP8X4),
                        lhsT_scale=w_scales[:, m, g * P : (g + 1) * P],
                        rhs=x_codes[half][:, g, first : first + width].bitcast(FP8X4),
                        rhs_scale=x_scales[half][:, g, first : first + width],
                        start=(g == 0),
                        stop=(g == PASSES - 1),
                    )
                nc.scalar.activation(
                    out=work["maps"][j][:, first : first + width],
                    in_=acc[:, 0:width],
                    func=ACT.Identity if m == VALUE_TILE else ACT.Relu,
                    bias=bias_t[:, m : m + 1],
                    scale=scale_t[:, m : m + 1],
                )

        def store_keys(work):
            half = work["half"]
            first = (half % 2) * HALF
            keys = [m for m in work["tiles"] if m != VALUE_TILE]
            nc.sync.dma_start(
                out=kf_view[half // 2, :, keys[0] : keys[-1] + 1, first : first + HALF],
                in_=work["kf"][:],
            )

        def slot_of(m):
            return 0 if m == VALUE_TILE else m + 1

        quads_of = {}
        sums_of = {}

        def quads_tile(half):
            if half not in quads_of:
                quads_of[half] = quads_pool.tile([P, TILES, QUADS], F32, name="quads")
            return quads_of[half]

        def sum_quads(work, j):
            pixels = work["maps"][j].rearrange("p (a r c d) -> p r d a c", r=2, c=24, d=2)
            acc = psum.tile([P, BANK], F32, tag="spare", bufs=1)
            for corner in range(4):
                nc.tensor.matmul(
                    acc[:, 0:QUADS].rearrange("p (a c) -> p a c", c=24),
                    lhsT=ident[:],
                    rhs=pixels[:, corner // 2, corner % 2],
                    start=(corner == 0),
                    stop=(corner == 3),
                )
            work["quads_acc"] = acc

        def sum_cells(work, j):
            b, part = divmod(work["half"], 2)
            slot = slot_of(work["tiles"][j])
            for sums, bands, size in zip(level_tiles(b)[2:], (3, 4), (4, 3)):
                nc.vector.tensor_reduce(
                    out=sums[:, slot, :].rearrange("p (h i c) -> p h i c", h=2, i=bands)[:, part],
                    in_=work["quads_acc"][:, 0:QUADS].rearrange(
                        "p (i r c w) -> p i c r w", i=bands, r=size, w=size
                    ),
                    axis=AXIS.XY,
                    op=ADD,
                )

        def vector_tiles(work):
            count = len(work["tiles"])
            if work["tiles"][0] == VALUE_TILE:
                return 1, count
            return 0, count - len(work["on_tensor"])

        def add_row_pairs(work):
            begin, end = vector_tiles(work)
            skip = 1 if work["tiles"][0] == VALUE_TILE else 0
            kf = work["kf"][:, begin - skip : end - skip, :]
            pairs = pool_tmp.tile([P, (end - begin) * HALF_ROWS // 2, SIDE], F32, name="row_pairs")
            rows = kf.rearrange("p n (a two w) -> p (n a) two w", two=2, w=SIDE)
            nc.vector.tensor_tensor(out=pairs[:], in0=rows[:, :, 0, :], in1=rows[:, :, 1, :], op=ADD)
            work["row_pairs"] = pairs

        def add_column_pairs(work):
            begin, end = vector_tiles(work)
            pairs = work["row_pairs"]
            cols = pairs[:].rearrange("p a (c two) -> p (a c) two", two=2)
            slot = slot_of(work["tiles"][begin])
            nc.vector.tensor_tensor(
                out=quads_tile(work["half"])[:, slot : slot + end - begin, :].rearrange("p n q -> p (n q)"),
                in0=cols[:, :, 0],
                in1=cols[:, :, 1],
                op=ADD,
            )

        def level_tiles(b):
            if b not in sums_of:
                sums_of[b] = [
                    sums_pool.tile([P, TILES, side * side], F32, name="level" + str(side))
                    for side in SIDES
                ]
            return sums_of[b]

        def cell_sums(half, first, last):
            n = last - first
            b, part = divmod(half, 2)
            quads = quads_of[half][:, first:last, :]
            sixes = quads.rearrange("p n (i s c) -> p (n i) s c", s=6, c=24)
            rows = quads.rearrange("p n (a c) -> p n a c", c=24)
            sums6, sums8 = level_tiles(b)[2:]
            two = band_pool.tile([P, n, 4, 24], F32, name="two")
            bands8 = band_pool.tile([P, n, 4, 24], F32, name="bands8")
            bands6 = band_pool.tile([P, n, 3, 24], F32, name="bands6")
            split = "p n (i j) c -> p (n i) j c"

            def add_two():
                nc.vector.tensor_tensor(
                    out=two[:].rearrange(split, j=2),
                    in0=sixes[:, :, 0:5:4, :],
                    in1=sixes[:, :, 1:6:4, :],
                    op=ADD,
                )

            def add_third():
                nc.vector.tensor_tensor(
                    out=bands8[:].rearrange(split, j=2),
                    in0=two[:].rearrange(split, j=2),
                    in1=sixes[:, :, 2:4, :],
                    op=ADD,
                )

            def middle_band():
                nc.vector.tensor_tensor(
                    out=bands6[:, :, 1, :], in0=two[:, :, 1, :], in1=two[:, :, 2, :], op=ADD
                )

            def outer_bands():
                nc.vector.tensor_tensor(
                    out=bands6[:, :, 0:3:2, :],
                    in0=bands8[:, :, 0:4:3, :],
                    in1=rows[:, :, 3:9:5, :],
                    op=ADD,
                )

            def level8():
                nc.vector.tensor_reduce(
                    out=sums8[:, first:last, 32 * part : 32 * (part + 1)],
                    in_=bands8[:].rearrange("p n r (c wi) -> p n (r c) wi", wi=3),
                    axis=AXIS.X,
                    op=ADD,
                )

            def level6():
                nc.vector.tensor_reduce(
                    out=sums6[:, first:last, 18 * part : 18 * (part + 1)],
                    in_=bands6[:].rearrange("p n r (c wi) -> p n (r c) wi", wi=4),
                    axis=AXIS.X,
                    op=ADD,
                )

            return [add_two, add_third, middle_band, outer_bands, level8, level6]

        def cell_sums_at_once(half, slot):
            b, part = divmod(half, 2)

            def level(sums, bands, size):
                def reduce():
                    nc.vector.tensor_reduce(
                        out=sums[:, slot, :].rearrange("p (h i c) -> p h i c", h=2, i=bands)[:, part],
                        in_=quads_of[half][:, slot, :].rearrange(
                            "p (i r c w) -> p i c r w", i=bands, r=size, w=size
                        ),
                        axis=AXIS.XY,
                        op=ADD,
                    )

                return reduce

            sums6, sums8 = level_tiles(b)[2:]
            return [level(sums6, 3, 4), level(sums8, 4, 3)]

        def means(b, first, last):
            sums1, sums3, sums6, sums8 = [sums[:, first:last, :] for sums in level_tiles(b)]
            tok = sums_pool.tile([P, last - first, TOKENS], F32, name="tok")

            def level3():
                nc.vector.tensor_reduce(
                    out=sums3.rearrange("p n (r c) -> p (n r) c", c=3),
                    in_=sums6.rearrange("p n (r hi c wi) -> p (n r) c hi wi", hi=2, c=3, wi=2),
                    axis=AXIS.XY,
                    op=ADD,
                )

            def whole():
                nc.vector.tensor_reduce(out=sums1, in_=sums6, axis=AXIS.X, op=ADD)

            def scale(sums, side, at):
                def multiply():
                    nc.vector.tensor_scalar_mul(
                        out=tok[:, :, at : at + side * side],
                        in0=sums,
                        scalar1=side * side / (SIDE * SIDE),
                    )

                return multiply

            def store_keys_means():
                skip = 1 if first == 0 else 0
                nc.sync.dma_start(
                    out=keyp_view[b, :, first + skip - 1 : last - 1, :], in_=tok[:, skip:, :]
                )

            def store_value():
                turned = psum.tile([P, BANK], F32, tag="spare", bufs=1)
                flat = tok[:].rearrange("p n t -> p (n t)")
                nc.tensor.transpose(turned[:, 0:P], flat[:, 0:P], ident[:])
                value = sums_pool.tile([P, P], F32, name="value")
                nc.scalar.copy(out=value[:], in_=turned[:, 0:P])
                nc.sync.dma_start(out=out_2[b], in_=value[0:TOKENS, :])

            steps = [
                scale(sums8, 8, AT8),
                level3,
                whole,
                scale(sums6, 6, AT6),
                scale(sums3, 3, AT3),
                scale(sums1, 1, 0),
            ]
            if first == 0:
                steps.append(store_value)
            return steps + [store_keys_means]

        groups = [[VALUE_TILE, 0, 1]] + [[m, m + 1] for m in range(2, KEY_TILES, 2)]
        last_groups = groups[:-1] + [[m] for m in groups[-1]]

        with tc.manual_schedule(engines={ENGINE.PE, ENGINE.Activation, ENGINE.DVE}):
            first_step = open_step(0, groups[0])
            near = 320
            far = 512
            for g in range(PASSES):
                regroup_x(0, g, 0, near, nc.vector.tensor_copy)
                regroup_x(0, g, near, BANK - near, nc.scalar.copy)
            turn_weights(VALUE_TILE)
            for g in range(PASSES):
                quantise_x(0, g, (BANK,))
            fold_norm()
            quantise_weights(VALUE_TILE)
            finish_norm()
            for m in groups[0][1:]:
                turn_weights(m)
                quantise_weights(m)
                if m == 0:
                    finish_bias()
            project(first_step, 0, BANK)
            for g in range(PASSES):
                regroup_x(0, g, BANK, far, nc.vector.tensor_copy, BANK)
                regroup_x(0, g, BANK + far, HALF - BANK - far, nc.scalar.copy, BANK)
            for g in range(PASSES):
                quantise_x(0, g, (BANK, HALF - 2 * BANK), BANK)

        due = []

        def work_off(count):
            for step in due[:count]:
                step()
            due[:count] = []

        blocks_of = tuple(
            tuple((step, block) for block in range(BLOCKS)) if step < PASSES else ()
            for step in range(len(groups))
        )

        previous = None
        for half in range(HALVES):
            following = half + 1
            burst = 3 if following < HALVES else 12
            for step, tiles in enumerate(groups if following < HALVES else last_groups):
                if half == 0 and step + 1 < len(groups):
                    for m in groups[step + 1]:
                        turn_weights(m)
                        quantise_weights(m)
                if half + 2 < HALVES and step < PASSES:
                    load_x(half + 2, step)
                if following < HALVES and 1 <= step <= PASSES:
                    quantise_x(following, step - 1, (2 * BANK, HALF - 2 * BANK))

                if half == 0 and step == 0:
                    work, begun = first_step, BANK
                else:
                    work, begun = open_step(half, tiles), 0
                for first in range(begun, HALF, BANK):
                    project(work, first, min(BANK, HALF - first))
                store_keys(work)

                if previous is not None and following == HALVES:
                    for j in previous["on_tensor"]:
                        sum_quads(previous, j)
                        sum_cells(previous, j)

                if previous is not None:
                    add_column_pairs(previous)
                work_off(burst)
                add_row_pairs(work)
                work_off(burst)
                if half > 0 and step == 0:
                    due.extend(cell_sums(half - 1, 5, 8 if (half - 1, 7) in TENSOR_TILES else TILES))
                    if half == 2:
                        due.extend(means(0, 0, TILES))
                if step == 2:
                    due.extend(cell_sums(half, 1, 4 if (half, 3) in TENSOR_TILES else 5))
                    if half == HALVES - 1:
                        due.extend(means(1, 0, 5))
                if half == HALVES - 1 and step == 3:
                    due.extend(cell_sums(half, 5, 7))
                if half == HALVES - 1 and step == 4:
                    due.extend(cell_sums_at_once(half, 7))
                finished, previous = previous, work

                if following < HALVES:
                    for g, block in blocks_of[step]:
                        on_vector = (g, block) in VECTOR_BLOCKS[following]
                        regroup_x(
                            following,
                            g,
                            block * BLOCK,
                            BLOCK,
                            nc.vector.tensor_copy if on_vector else nc.scalar.copy,
                        )
                    if finished is not None:
                        for j in finished["on_tensor"]:
                            sum_quads(finished, j)
                            sum_cells(finished, j)

        add_column_pairs(previous)
        due.extend(cell_sums_at_once(HALVES - 1, TILES - 1))
        due.extend(means(1, 5, TILES))
        work_off(len(due))
